import numpy as np
import ml_dtypes

BF16 = ml_dtypes.bfloat16


def bf(x):
    return np.asarray(x, np.float32).astype(BF16)


def f32(x):
    return np.asarray(x, np.float32)


def f64(x):
    return np.asarray(x).astype(np.float64)


def striped(idx):
    return np.tile(idx.reshape(-1, 16).T, (8, 1))


C, S, N, B, T, H, DH, E, F = 512, 4096, 1024, 2, 512, 4, 128, 1536, 2048
EPS = 1e-5


def erf(a):
    c = np.clip(a, -6.0, 6.0)
    term = c.copy()
    total = c.copy()
    for n in range(1, 150):
        term = term * (2.0 * c * c) / (2.0 * n + 1.0)
        total = total + term
    r = 2.0 / np.sqrt(np.pi) * np.exp(-c * c) * total
    return np.where(np.abs(a) > 6.0, np.sign(a), r)


def gelu_erf(v):
    return 0.5 * v * (1.0 + erf(v / np.sqrt(2.0)))


def layernorm(v, w, b):
    mu = v.mean(axis=0, keepdims=True)
    var = np.square(v - mu).mean(axis=0, keepdims=True)
    return (v - mu) / np.sqrt(var + EPS) * w + b


def setup_inputs():
    return {
        "tok_emb": f32(0.7 * np.random.standard_normal((C, S))),
        "pos_emb": f32(0.7 * np.random.standard_normal((C, T))),
        "ln1_w": f32(1.0 + 0.1 * np.random.standard_normal((C, 1))),
        "ln1_b": f32(0.1 * np.random.standard_normal((C, 1))),
        "qkv_w": bf(1.25 * np.random.standard_normal((C, E)) / np.sqrt(C)),
        "proj_w": bf(np.random.standard_normal((C, C)) / np.sqrt(C)),
        "ln2_w": f32(1.0 + 0.1 * np.random.standard_normal((C, 1))),
        "ln2_b": f32(0.1 * np.random.standard_normal((C, 1))),
        "fc1_w": bf(np.random.standard_normal((C, F)) / np.sqrt(C)),
        "fc2_w": bf(np.random.standard_normal((F, C)) / np.sqrt(F)),
        "offs": striped(np.random.permutation(np.tile(np.arange(S), 2))[:N]),
    }


def reference(tok_emb, pos_emb, ln1_w, ln1_b, qkv_w, proj_w, ln2_w, ln2_b, fc1_w, fc2_w, offs):
    idx = offs[:16].T.reshape(-1)
    h = f64(tok_emb)[:, idx] + np.tile(f64(pos_emb), (1, B))
    n1 = layernorm(h, f64(ln1_w), f64(ln1_b))
    q, k, v = np.split(f64(qkv_w).T @ n1, E // C, axis=0)
    q = q.reshape(H, DH, B, T)
    k = k.reshape(H, DH, B, T)
    v = v.reshape(H, DH, B, T)
    sc = np.einsum('hdbt,hdbu->hbtu', q, k) / np.sqrt(DH)
    sc = np.where(np.tril(np.ones((T, T), bool)), sc, -np.inf)
    p = np.exp(sc - sc.max(axis=-1, keepdims=True))
    p = p / p.sum(axis=-1, keepdims=True)
    o = np.einsum('hbtu,hdbu->hdbt', p, v).reshape(C, N)
    h = h + f64(proj_w).T @ o
    n2 = layernorm(h, f64(ln2_w), f64(ln2_b))
    u = gelu_erf(f64(fc1_w).T @ n2)
    return h + f64(fc2_w).T @ u

@@ -1,0 +1,232 @@
+import math
+from contextlib import ExitStack
+
+import concourse.mybir as mybir
+from concourse.masks import make_identity
+
+F32 = mybir.dt.float32
+BF16 = mybir.dt.bfloat16
+U16 = mybir.dt.uint16
+I32 = mybir.dt.int32
+ALU = mybir.AluOpType
+FN = mybir.ActivationFunctionType
+AXIS_X = mybir.AxisListType.X
+
+P = 128
+C, S, N, B, T, H, DH, E, F = 512, 4096, 1024, 2, 512, 4, 128, 1536, 2048
+CB = C // P
+FB = F // P
+TB = T // P
+EPS = 1e-5
+MASKED = -1e30
+
+FLOPS = 2 * N * C * E + 4 * B * H * DH * (T * (T + 1) // 2) + 2 * N * C * C + 4 * N * C * F
+
+
+def tile_tinygpt_ntp_b_kernel(
+    tc, tok_emb, pos_emb, ln1_w, ln1_b, qkv_w, proj_w, ln2_w, ln2_b, fc1_w, fc2_w, offs, out
+):
+    nc = tc.nc
+    with ExitStack() as pools:
+        held = pools.enter_context(tc.tile_pool(name="held", bufs=1))
+        norm = pools.enter_context(tc.tile_pool(name="norm", bufs=2))
+        acc = pools.enter_context(tc.psum_pool(name="acc", bufs=4))
+
+        offsets = held.tile([P, N // 16], U16, name="offsets")
+        nc.sync.dma_start(offsets[:], offs)
+
+        ident = held.tile([P, P], BF16, name="ident")
+        make_identity(nc, ident[:])
+        ident64 = held.tile([64, 64], F32, name="ident64")
+        make_identity(nc, ident64[:])
+        ahead = held.tile([P, P], I32, name="ahead")
+        nc.gpsimd.iota(ahead[:], pattern=[[1, P]], base=0, channel_multiplier=-1)
+        causal = held.tile([P, P], BF16, name="causal")
+        nc.vector.tensor_scalar(causal[:], ahead[:], 0.0, MASKED, op0=ALU.is_gt, op1=ALU.mult)
+        averager = held.tile([P, P], BF16, name="averager")
+        nc.vector.memset(averager[:], 1.0 / C)
+        eps = held.tile([P, 1], F32, name="eps")
+        nc.vector.memset(eps[:], EPS)
+
+        ln_rows = held.tile([64, P], F32, name="ln_rows")
+        nc.vector.memset(ln_rows[:], 0.0)
+        for v, vec in enumerate((ln1_w, ln1_b, ln2_w, ln2_b)):
+            nc.scalar.dma_start(
+                ln_rows[v * CB : (v + 1) * CB, :], vec.rearrange("(cb p) o -> cb (p o)", p=P)
+            )
+        ln_ps = acc.tile([P, T], F32, name="ln_ps", tag="acc")
+        nc.tensor.transpose(ln_ps[:, 0:64], ln_rows[:], ident64[:])
+        ln_cols = held.tile([P, 4 * CB], F32, name="ln_cols")
+        nc.vector.tensor_copy(ln_cols[:], ln_ps[:, 0 : 4 * CB])
+
+        h0 = held.tile([P, CB, N], F32, name="h0")
+        qkv_sb = held.tile([P, CB, E], BF16, name="qkv_sb")
+        proj_sb = held.tile([P, CB, C], BF16, name="proj_sb")
+        fc1_sb = held.tile([P, CB, F], BF16, name="fc1_sb")
+        fc2_sb = held.tile([P, FB, C], BF16, name="fc2_sb")
+        with tc.tile_pool(name="table", bufs=1) as table:
+            pos_sb = table.tile([P, CB, T], F32, name="pos_sb")
+            nc.scalar.dma_start(pos_sb[:], pos_emb.rearrange("(cb p) t -> p cb t", p=P))
+            tok = []
+            for cb in range(CB):
+                tok_cb = table.tile([P, S], F32, name=f"tok{cb}")
+                nc.sync.dma_start(tok_cb[:], tok_emb[cb * P : (cb + 1) * P, :])
+                tok.append(tok_cb)
+            nc.sync.dma_start(qkv_sb[:], qkv_w.rearrange("(cb p) e -> p cb e", p=P))
+            nc.sync.dma_start(proj_sb[:], proj_w.rearrange("(cb p) c -> p cb c", p=P))
+            nc.sync.dma_start(fc1_sb[:], fc1_w.rearrange("(cb p) f -> p cb f", p=P))
+            nc.sync.dma_start(fc2_sb[:], fc2_w.rearrange("(fb p) c -> p fb c", p=P))
+            for s in range(B):
+                for cb in range(CB):
+                    nc.vector.tensor_tensor(
+                        h0[:, cb, s * T : (s + 1) * T],
+                        tok[cb][:].indirect(offsets[:, s * (T // 16) : (s + 1) * (T // 16)]),
+                        pos_sb[:, cb, :],
+                        ALU.add,
+                    )
+
+        late = pools.enter_context(tc.tile_pool(name="late", bufs=1))
+        h1 = late.tile([P, CB, N], F32, name="h1")
+
+        def layer_norm(x, s, v):
+            cols = slice(s * T, (s + 1) * T)
+            mean = acc.tile([P, T], F32, name="mean", tag="acc")
+            for cb in range(CB):
+                xb = norm.tile([P, T], BF16, name="xb", bufs=4)
+                nc.gpsimd.tensor_copy(xb[:], x[:, cb, cols])
+                nc.tensor.matmul(mean[:], averager[:], xb[:], start=(cb == 0), stop=(cb == CB - 1))
+            xc = norm.tile([P, CB, T], F32, name="xc")
+            var = acc.tile([P, T], F32, name="var", tag="acc")
+            for cb in range(CB):
+                nc.vector.tensor_tensor(xc[:, cb, :], x[:, cb, cols], mean[:], ALU.subtract)
+                sq = norm.tile([P, T], BF16, name="sq", bufs=4)
+                nc.scalar.square(sq[:], xc[:, cb, :])
+                nc.tensor.matmul(var[:], averager[:], sq[:], start=(cb == 0), stop=(cb == CB - 1))
+            logv = norm.tile([P, T], F32, name="logv")
+            nc.scalar.activation(logv[:], var[:], FN.Ln, bias=eps[:, 0:1])
+            rstd = norm.tile([P, T], F32, name="rstd")
+            nc.scalar.activation(rstd[:], logv[:], FN.Exp, scale=-0.5)
+            n = norm.tile([P, CB, T], BF16, name="n")
+            for cb in range(CB):
+                xn = norm.tile([P, T], F32, name="xn", bufs=4)
+                nc.vector.tensor_tensor(xn[:], xc[:, cb, :], rstd[:], ALU.mult)
+                nc.gpsimd.tensor_scalar(
+                    n[:, cb, :], xn[:],
+                    ln_cols[:, v * CB + cb : v * CB + cb + 1],
+                    ln_cols[:, (v + 1) * CB + cb : (v + 1) * CB + cb + 1],
+                    op0=ALU.mult, op1=ALU.add,
+                )
+            return n
+
+        n1 = [layer_norm(h0, s, 0) for s in range(B)]
+        n2 = []
+
+        with ExitStack() as attention_pools:
+            soft = attention_pools.enter_context(tc.tile_pool(name="soft", bufs=3))
+            att_ps = attention_pools.enter_context(tc.psum_pool(name="att_ps", bufs=1))
+            for s in range(B):
+                cols = slice(s * T, (s + 1) * T)
+                q = late.tile([P, H, T], BF16, name=f"q{s}")
+                k = late.tile([P, H, T], BF16, name=f"k{s}")
+                v_t = late.tile([P, TB, C], BF16, name=f"v_t{s}")
+                o = late.tile([P, H, T], BF16, name=f"o{s}")
+                for head in range(H):
+                    q_ps = acc.tile([P, T], F32, name="q_ps", tag="acc")
+                    for cb in range(CB):
+                        nc.tensor.matmul(
+                            q_ps[:], qkv_sb[:, cb, head * DH : (head + 1) * DH], n1[s][:, cb, :],
+                            start=(cb == 0), stop=(cb == CB - 1),
+                        )
+                    nc.scalar.mul(q[:, head, :], q_ps[:], 1.0 / math.sqrt(DH))
+                    k_ps = acc.tile([P, T], F32, name="k_ps", tag="acc")
+                    for cb in range(CB):
+                        nc.tensor.matmul(
+                            k_ps[:], qkv_sb[:, cb, C + head * DH : C + (head + 1) * DH], n1[s][:, cb, :],
+                            start=(cb == 0), stop=(cb == CB - 1),
+                        )
+                    nc.scalar.copy(k[:, head, :], k_ps[:])
+
+                    p_t = soft.tile([P, TB, T], BF16, name="p_t", bufs=2)
+                    for jb in range(TB):
+                        seen = jb * P
+                        width = seen + P
+                        q_blk = q[:, head, seen:width]
+                        sc = att_ps.tile([P, T], F32, name="sc", bufs=2)
+                        if jb > 0:
+                            nc.tensor.matmul(sc[:, 0:seen], q_blk, k[:, head, 0:seen], start=True, stop=True)
+                        nc.tensor.matmul(sc[:, seen:width], ident[:], causal[:], start=True, stop=False)
+                        nc.tensor.matmul(sc[:, seen:width], q_blk, k[:, head, seen:width], start=False, stop=True)
+                        neg_max = soft.tile([P, 1], F32, name="neg_max")
+                        nc.vector.reduce_max(neg_max[:], sc[:, 0:width], axis=AXIS_X, negate=True)
+                        e = soft.tile([P, T], F32, name="e")
+                        e_sum = soft.tile([P, 1], F32, name="e_sum")
+                        nc.scalar.activation(
+                            e[:, 0:width], sc[:, 0:width], FN.Exp, bias=neg_max[:, 0:1], accum_out=e_sum[:, 0:1]
+                        )
+                        inv_sum = soft.tile([P, 1], F32, name="inv_sum")
+                        nc.vector.reciprocal(inv_sum[:], e_sum[:])
+                        p = soft.tile([P, T], BF16, name="p")
+                        nc.gpsimd.tensor_scalar(
+                            p[:, 0:width], e[:, 0:width], inv_sum[:, 0:1], 1.0, op0=ALU.mult, op1=ALU.mult
+                        )
+                        pt_ps = att_ps.tile([P, T], BF16, name="pt_ps")
+                        for ib in range(jb + 1):
+                            nc.tensor.transpose(pt_ps[:, ib * P : (ib + 1) * P], p[:, ib * P : (ib + 1) * P], ident[:])
+                        nc.vector.tensor_copy(
+                            p_t[:, 0 : jb + 1, seen:width],
+                            pt_ps[:, 0:width].rearrange("i (ib j) -> i ib j", j=P),
+                        )
+
+                    if head == 0:
+                        for tb in range(TB):
+                            v_ps = acc.tile([P, C], F32, name="v_ps", tag="acc")
+                            for cb in range(CB):
+                                nc.tensor.matmul(
+                                    v_ps[:], n1[s][:, cb, tb * P : (tb + 1) * P], qkv_sb[:, cb, 2 * C : 3 * C],
+                                    start=(cb == 0), stop=(cb == CB - 1),
+                                )
+                            nc.scalar.copy(v_t[:, tb, :], v_ps[:])
+
+                    o_ps = att_ps.tile([P, T], F32, name="o_ps")
+                    for ib in range(TB):
+                        nc.tensor.matmul(
+                            o_ps[:, ib * P : T], v_t[:, ib, head * DH : (head + 1) * DH], p_t[:, ib, ib * P : T],
+                            start=(ib == 0), stop=(ib == TB - 1),
+                        )
+                    nc.scalar.copy(o[:, head, :], o_ps[:])
+
+                for cb in range(CB):
+                    h_ps = acc.tile([P, T], F32, name="h_ps", tag="acc")
+                    for head in range(H):
+                        nc.tensor.matmul(
+                            h_ps[:], proj_sb[:, head, cb * P : (cb + 1) * P], o[:, head, :],
+                            start=(head == 0), stop=(head == H - 1),
+                        )
+                    nc.vector.tensor_tensor(h1[:, cb, cols], h0[:, cb, cols], h_ps[:], ALU.add)
+                n2.append(layer_norm(h1, s, 2))
+
+        with tc.psum_pool(name="mlp_ps", bufs=4) as mlp_ps:
+            u = []
+            for s in range(B):
+                u_s = late.tile([P, FB, T], BF16, name=f"u{s}")
+                for fb in range(FB):
+                    u_ps = mlp_ps.tile([P, T], F32, name="u_ps", tag="mlp")
+                    for cb in range(CB):
+                        nc.tensor.matmul(
+                            u_ps[:], fc1_sb[:, cb, fb * P : (fb + 1) * P], n2[s][:, cb, :],
+                            start=(cb == 0), stop=(cb == CB - 1),
+                        )
+                    nc.scalar.activation(u_s[:, fb, :], u_ps[:], FN.Gelu)
+                u.append(u_s)
+            for s in range(B):
+                cols = slice(s * T, (s + 1) * T)
+                for cb in range(CB):
+                    y_ps = mlp_ps.tile([P, T], F32, name="y_ps", tag="mlp")
+                    for fb in range(FB):
+                        nc.tensor.matmul(
+                            y_ps[:], fc2_sb[:, fb, cb * P : (cb + 1) * P], u[s][:, fb, :],
+                            start=(fb == 0), stop=(fb == FB - 1),
+                        )
+                    y = late.tile([P, T], F32, name="y", bufs=3)
+                    nc.vector.tensor_tensor(y[:], h1[:, cb, cols], y_ps[:], ALU.add)
+                    nc.sync.dma_start(out[cb * P : (cb + 1) * P, cols], y[:])

@@ -30,7 +30,7 @@ def tile_tinygpt_ntp_b_kernel(
     with ExitStack() as pools:
         held = pools.enter_context(tc.tile_pool(name="held", bufs=1))
         norm = pools.enter_context(tc.tile_pool(name="norm", bufs=2))
-        acc = pools.enter_context(tc.psum_pool(name="acc", bufs=4))
+        stat_ps = pools.enter_context(tc.psum_pool(name="stat_ps", bufs=2))
 
         offsets = held.tile([P, N // 16], U16, name="offsets")
         nc.sync.dma_start(offsets[:], offs)
@@ -48,18 +48,8 @@ def tile_tinygpt_ntp_b_kernel(
         eps = held.tile([P, 1], F32, name="eps")
         nc.vector.memset(eps[:], EPS)
 
-        ln_rows = held.tile([64, P], F32, name="ln_rows")
-        nc.vector.memset(ln_rows[:], 0.0)
-        for v, vec in enumerate((ln1_w, ln1_b, ln2_w, ln2_b)):
-            nc.scalar.dma_start(
-                ln_rows[v * CB : (v + 1) * CB, :], vec.rearrange("(cb p) o -> cb (p o)", p=P)
-            )
-        ln_ps = acc.tile([P, T], F32, name="ln_ps", tag="acc")
-        nc.tensor.transpose(ln_ps[:, 0:64], ln_rows[:], ident64[:])
-        ln_cols = held.tile([P, 4 * CB], F32, name="ln_cols")
-        nc.vector.tensor_copy(ln_cols[:], ln_ps[:, 0 : 4 * CB])
-
         h0 = held.tile([P, CB, N], F32, name="h0")
+        ln_rows = held.tile([64, P], F32, name="ln_rows")
         qkv_sb = held.tile([P, CB, E], BF16, name="qkv_sb")
         proj_sb = held.tile([P, CB, C], BF16, name="proj_sb")
         fc1_sb = held.tile([P, CB, F], BF16, name="fc1_sb")
@@ -76,6 +66,11 @@ def tile_tinygpt_ntp_b_kernel(
             nc.sync.dma_start(proj_sb[:], proj_w.rearrange("(cb p) c -> p cb c", p=P))
             nc.sync.dma_start(fc1_sb[:], fc1_w.rearrange("(cb p) f -> p cb f", p=P))
             nc.sync.dma_start(fc2_sb[:], fc2_w.rearrange("(fb p) c -> p fb c", p=P))
+            nc.vector.memset(ln_rows[:], 0.0)
+            for v, vec in enumerate((ln1_w, ln1_b, ln2_w, ln2_b)):
+                nc.scalar.dma_start(
+                    ln_rows[v * CB : (v + 1) * CB, :], vec.rearrange("(cb p) o -> cb (p o)", p=P)
+                )
             for s in range(B):
                 for cb in range(CB):
                     nc.vector.tensor_tensor(
@@ -85,22 +80,27 @@ def tile_tinygpt_ntp_b_kernel(
                         ALU.add,
                     )
 
+        ln_ps = stat_ps.tile([P, T], F32, name="ln_ps", tag="stat")
+        nc.tensor.transpose(ln_ps[:, 0:64], ln_rows[:], ident64[:])
+        ln_cols = held.tile([P, 4 * CB], F32, name="ln_cols")
+        nc.vector.tensor_copy(ln_cols[:], ln_ps[:, 0 : 4 * CB])
+
         late = pools.enter_context(tc.tile_pool(name="late", bufs=1))
         h1 = late.tile([P, CB, N], F32, name="h1")
 
         def layer_norm(x, s, v):
             cols = slice(s * T, (s + 1) * T)
-            mean = acc.tile([P, T], F32, name="mean", tag="acc")
+            mean = stat_ps.tile([P, T], F32, name="mean", tag="stat")
             for cb in range(CB):
                 xb = norm.tile([P, T], BF16, name="xb", bufs=4)
                 nc.gpsimd.tensor_copy(xb[:], x[:, cb, cols])
                 nc.tensor.matmul(mean[:], averager[:], xb[:], start=(cb == 0), stop=(cb == CB - 1))
             xc = norm.tile([P, CB, T], F32, name="xc")
-            var = acc.tile([P, T], F32, name="var", tag="acc")
+            var = stat_ps.tile([P, T], F32, name="var", tag="stat")
             for cb in range(CB):
                 nc.vector.tensor_tensor(xc[:, cb, :], x[:, cb, cols], mean[:], ALU.subtract)
                 sq = norm.tile([P, T], BF16, name="sq", bufs=4)
-                nc.scalar.square(sq[:], xc[:, cb, :])
+                nc.vector.tensor_tensor(sq[:], xc[:, cb, :], xc[:, cb, :], ALU.mult)
                 nc.tensor.matmul(var[:], averager[:], sq[:], start=(cb == 0), stop=(cb == CB - 1))
             logv = norm.tile([P, T], F32, name="logv")
             nc.scalar.activation(logv[:], var[:], FN.Ln, bias=eps[:, 0:1])
@@ -108,14 +108,14 @@ def tile_tinygpt_ntp_b_kernel(
             nc.scalar.activation(rstd[:], logv[:], FN.Exp, scale=-0.5)
             n = norm.tile([P, CB, T], BF16, name="n")
             for cb in range(CB):
+                gain = ln_cols[:, v * CB + cb : v * CB + cb + 1]
+                bias = ln_cols[:, (v + 1) * CB + cb : (v + 1) * CB + cb + 1]
                 xn = norm.tile([P, T], F32, name="xn", bufs=4)
                 nc.vector.tensor_tensor(xn[:], xc[:, cb, :], rstd[:], ALU.mult)
-                nc.gpsimd.tensor_scalar(
-                    n[:, cb, :], xn[:],
-                    ln_cols[:, v * CB + cb : v * CB + cb + 1],
-                    ln_cols[:, (v + 1) * CB + cb : (v + 1) * CB + cb + 1],
-                    op0=ALU.mult, op1=ALU.add,
-                )
+                if cb % 2 == 0:
+                    nc.gpsimd.tensor_scalar(n[:, cb, :], xn[:], gain, bias, op0=ALU.mult, op1=ALU.add)
+                else:
+                    nc.scalar.activation(n[:, cb, :], xn[:], FN.Identity, bias=bias, scale=gain)
             return n
 
         n1 = [layer_norm(h0, s, 0) for s in range(B)]
@@ -123,80 +123,94 @@ def tile_tinygpt_ntp_b_kernel(
 
         with ExitStack() as attention_pools:
             soft = attention_pools.enter_context(tc.tile_pool(name="soft", bufs=3))
+            qkv_ps = attention_pools.enter_context(tc.psum_pool(name="qkv_ps", bufs=2))
             att_ps = attention_pools.enter_context(tc.psum_pool(name="att_ps", bufs=1))
+
+            def project_qk(s, head, q, k):
+                q_ps = qkv_ps.tile([P, T], F32, name="q_ps", tag="qkv")
+                for cb in range(CB):
+                    nc.tensor.matmul(
+                        q_ps[:], qkv_sb[:, cb, head * DH : (head + 1) * DH], n1[s][:, cb, :],
+                        start=(cb == 0), stop=(cb == CB - 1),
+                    )
+                nc.scalar.mul(q[:, head, :], q_ps[:], 1.0 / math.sqrt(DH))
+                k_ps = qkv_ps.tile([P, T], F32, name="k_ps", tag="qkv")
+                for cb in range(CB):
+                    nc.tensor.matmul(
+                        k_ps[:], qkv_sb[:, cb, C + head * DH : C + (head + 1) * DH], n1[s][:, cb, :],
+                        start=(cb == 0), stop=(cb == CB - 1),
+                    )
+                nc.scalar.copy(k[:, head, :], k_ps[:])
+
+            def project_v(s, v_t):
+                for tb in range(TB):
+                    v_ps = qkv_ps.tile([P, C], F32, name="v_ps", tag="qkv")
+                    for cb in range(CB):
+                        nc.tensor.matmul(
+                            v_ps[:], n1[s][:, cb, tb * P : (tb + 1) * P], qkv_sb[:, cb, 2 * C : 3 * C],
+                            start=(cb == 0), stop=(cb == CB - 1),
+                        )
+                    nc.scalar.copy(v_t[:, tb, :], v_ps[:])
+
+            def softmax_weights(head, q, k):
+                p_t = soft.tile([P, TB, T], BF16, name="p_t", bufs=2)
+                for jb in range(TB):
+                    seen = jb * P
+                    width = seen + P
+                    q_blk = q[:, head, seen:width]
+                    sc = att_ps.tile([P, T], F32, name="sc", bufs=2)
+                    if jb > 0:
+                        nc.tensor.matmul(sc[:, 0:seen], q_blk, k[:, head, 0:seen], start=True, stop=True)
+                    nc.tensor.matmul(sc[:, seen:width], ident[:], causal[:], start=True, stop=False)
+                    nc.tensor.matmul(sc[:, seen:width], q_blk, k[:, head, seen:width], start=False, stop=True)
+                    neg_max = soft.tile([P, 1], F32, name="neg_max")
+                    nc.vector.reduce_max(neg_max[:], sc[:, 0:width], axis=AXIS_X, negate=True)
+                    e = soft.tile([P, T], F32, name="e")
+                    e_sum = soft.tile([P, 1], F32, name="e_sum")
+                    nc.scalar.activation(
+                        e[:, 0:width], sc[:, 0:width], FN.Exp, bias=neg_max[:, 0:1], accum_out=e_sum[:, 0:1]
+                    )
+                    inv_sum = soft.tile([P, 1], F32, name="inv_sum")
+                    nc.vector.reciprocal(inv_sum[:], e_sum[:])
+                    p = soft.tile([P, T], BF16, name="p")
+                    nc.gpsimd.tensor_scalar(
+                        p[:, 0:width], e[:, 0:width], inv_sum[:, 0:1], 1.0, op0=ALU.mult, op1=ALU.mult
+                    )
+                    pt_ps = att_ps.tile([P, T], BF16, name="pt_ps")
+                    for ib in range(jb + 1):
+                        nc.tensor.transpose(pt_ps[:, ib * P : (ib + 1) * P], p[:, ib * P : (ib + 1) * P], ident[:])
+                    nc.vector.tensor_copy(
+                        p_t[:, 0 : jb + 1, seen:width],
+                        pt_ps[:, 0:width].rearrange("i (ib j) -> i ib j", j=P),
+                    )
+                return p_t
+
+            def weighted_values(head, v_t, p_t, o):
+                o_ps = att_ps.tile([P, T], F32, name="o_ps")
+                for ib in range(TB):
+                    nc.tensor.matmul(
+                        o_ps[:, ib * P : T], v_t[:, ib, head * DH : (head + 1) * DH], p_t[:, ib, ib * P : T],
+                        start=(ib == 0), stop=(ib == TB - 1),
+                    )
+                nc.scalar.copy(o[:, head, :], o_ps[:])
+
             for s in range(B):
                 cols = slice(s * T, (s + 1) * T)
                 q = late.tile([P, H, T], BF16, name=f"q{s}")
                 k = late.tile([P, H, T], BF16, name=f"k{s}")
                 v_t = late.tile([P, TB, C], BF16, name=f"v_t{s}")
                 o = late.tile([P, H, T], BF16, name=f"o{s}")
+                project_qk(s, 0, q, k)
                 for head in range(H):
-                    q_ps = acc.tile([P, T], F32, name="q_ps", tag="acc")
-                    for cb in range(CB):
-                        nc.tensor.matmul(
-                            q_ps[:], qkv_sb[:, cb, head * DH : (head + 1) * DH], n1[s][:, cb, :],
-                            start=(cb == 0), stop=(cb == CB - 1),
-                        )
-                    nc.scalar.mul(q[:, head, :], q_ps[:], 1.0 / math.sqrt(DH))
-                    k_ps = acc.tile([P, T], F32, name="k_ps", tag="acc")
-                    for cb in range(CB):
-                        nc.tensor.matmul(
-                            k_ps[:], qkv_sb[:, cb, C + head * DH : C + (head + 1) * DH], n1[s][:, cb, :],
-                            start=(cb == 0), stop=(cb == CB - 1),
-                        )
-                    nc.scalar.copy(k[:, head, :], k_ps[:])
-
-                    p_t = soft.tile([P, TB, T], BF16, name="p_t", bufs=2)
-                    for jb in range(TB):
-                        seen = jb * P
-                        width = seen + P
-                        q_blk = q[:, head, seen:width]
-                        sc = att_ps.tile([P, T], F32, name="sc", bufs=2)
-                        if jb > 0:
-                            nc.tensor.matmul(sc[:, 0:seen], q_blk, k[:, head, 0:seen], start=True, stop=True)
-                        nc.tensor.matmul(sc[:, seen:width], ident[:], causal[:], start=True, stop=False)
-                        nc.tensor.matmul(sc[:, seen:width], q_blk, k[:, head, seen:width], start=False, stop=True)
-                        neg_max = soft.tile([P, 1], F32, name="neg_max")
-                        nc.vector.reduce_max(neg_max[:], sc[:, 0:width], axis=AXIS_X, negate=True)
-                        e = soft.tile([P, T], F32, name="e")
-                        e_sum = soft.tile([P, 1], F32, name="e_sum")
-                        nc.scalar.activation(
-                            e[:, 0:width], sc[:, 0:width], FN.Exp, bias=neg_max[:, 0:1], accum_out=e_sum[:, 0:1]
-                        )
-                        inv_sum = soft.tile([P, 1], F32, name="inv_sum")
-                        nc.vector.reciprocal(inv_sum[:], e_sum[:])
-                        p = soft.tile([P, T], BF16, name="p")
-                        nc.gpsimd.tensor_scalar(
-                            p[:, 0:width], e[:, 0:width], inv_sum[:, 0:1], 1.0, op0=ALU.mult, op1=ALU.mult
-                        )
-                        pt_ps = att_ps.tile([P, T], BF16, name="pt_ps")
-                        for ib in range(jb + 1):
-                            nc.tensor.transpose(pt_ps[:, ib * P : (ib + 1) * P], p[:, ib * P : (ib + 1) * P], ident[:])
-                        nc.vector.tensor_copy(
-                            p_t[:, 0 : jb + 1, seen:width],
-                            pt_ps[:, 0:width].rearrange("i (ib j) -> i ib j", j=P),
-                        )
-
+                    p_t = softmax_weights(head, q, k)
                     if head == 0:
-                        for tb in range(TB):
-                            v_ps = acc.tile([P, C], F32, name="v_ps", tag="acc")
-                            for cb in range(CB):
-                                nc.tensor.matmul(
-                                    v_ps[:], n1[s][:, cb, tb * P : (tb + 1) * P], qkv_sb[:, cb, 2 * C : 3 * C],
-                                    start=(cb == 0), stop=(cb == CB - 1),
-                                )
-                            nc.scalar.copy(v_t[:, tb, :], v_ps[:])
-
-                    o_ps = att_ps.tile([P, T], F32, name="o_ps")
-                    for ib in range(TB):
-                        nc.tensor.matmul(
-                            o_ps[:, ib * P : T], v_t[:, ib, head * DH : (head + 1) * DH], p_t[:, ib, ib * P : T],
-                            start=(ib == 0), stop=(ib == TB - 1),
-                        )
-                    nc.scalar.copy(o[:, head, :], o_ps[:])
+                        project_v(s, v_t)
+                    if head + 1 < H:
+                        project_qk(s, head + 1, q, k)
+                    weighted_values(head, v_t, p_t, o)
 
                 for cb in range(CB):
-                    h_ps = acc.tile([P, T], F32, name="h_ps", tag="acc")
+                    h_ps = stat_ps.tile([P, T], F32, name="h_ps", tag="stat")
                     for head in range(H):
                         nc.tensor.matmul(
                             h_ps[:], proj_sb[:, head, cb * P : (cb + 1) * P], o[:, head, :],
@@ -205,10 +219,10 @@ def tile_tinygpt_ntp_b_kernel(
                     nc.vector.tensor_tensor(h1[:, cb, cols], h0[:, cb, cols], h_ps[:], ALU.add)
                 n2.append(layer_norm(h1, s, 2))
 
-        with tc.psum_pool(name="mlp_ps", bufs=4) as mlp_ps:
-            u = []
+        with tc.psum_pool(name="mlp_ps", bufs=6) as mlp_ps:
             for s in range(B):
-                u_s = late.tile([P, FB, T], BF16, name=f"u{s}")
+                cols = slice(s * T, (s + 1) * T)
+                u = late.tile([P, FB, T], BF16, name=f"u{s}")
                 for fb in range(FB):
                     u_ps = mlp_ps.tile([P, T], F32, name="u_ps", tag="mlp")
                     for cb in range(CB):
@@ -216,15 +230,12 @@ def tile_tinygpt_ntp_b_kernel(
                             u_ps[:], fc1_sb[:, cb, fb * P : (fb + 1) * P], n2[s][:, cb, :],
                             start=(cb == 0), stop=(cb == CB - 1),
                         )
-                    nc.scalar.activation(u_s[:, fb, :], u_ps[:], FN.Gelu)
-                u.append(u_s)
-            for s in range(B):
-                cols = slice(s * T, (s + 1) * T)
+                    nc.scalar.activation(u[:, fb, :], u_ps[:], FN.Gelu)
                 for cb in range(CB):
                     y_ps = mlp_ps.tile([P, T], F32, name="y_ps", tag="mlp")
                     for fb in range(FB):
                         nc.tensor.matmul(
-                            y_ps[:], fc2_sb[:, fb, cb * P : (cb + 1) * P], u[s][:, fb, :],
+                            y_ps[:], fc2_sb[:, fb, cb * P : (cb + 1) * P], u[:, fb, :],
                             start=(fb == 0), stop=(fb == FB - 1),
                         )
                     y = late.tile([P, T], F32, name="y", bufs=3)

@@ -47,6 +47,8 @@ def tile_tinygpt_ntp_b_kernel(
         nc.vector.memset(averager[:], 1.0 / C)
         eps = held.tile([P, 1], F32, name="eps")
         nc.vector.memset(eps[:], EPS)
+        warm = held.tile([P, 1], F32, name="warm")
+        nc.scalar.activation(warm[:], eps[:], FN.Abs_reciprocal_sqrt)
 
         h0 = held.tile([P, CB, N], F32, name="h0")
         ln_rows = held.tile([64, P], F32, name="ln_rows")
@@ -90,22 +92,22 @@ def tile_tinygpt_ntp_b_kernel(
 
         def layer_norm(x, s, v):
             cols = slice(s * T, (s + 1) * T)
+            part = norm.tile([P, T], F32, name="part")
+            nc.vector.tensor_tensor(part[:], x[:, 0, cols], x[:, 1, cols], ALU.add)
+            nc.vector.tensor_tensor(part[:], part[:], x[:, 2, cols], ALU.add)
+            total = norm.tile([P, T], BF16, name="total")
+            nc.vector.tensor_tensor(total[:], part[:], x[:, 3, cols], ALU.add)
             mean = stat_ps.tile([P, T], F32, name="mean", tag="stat")
-            for cb in range(CB):
-                xb = norm.tile([P, T], BF16, name="xb", bufs=4)
-                nc.gpsimd.tensor_copy(xb[:], x[:, cb, cols])
-                nc.tensor.matmul(mean[:], averager[:], xb[:], start=(cb == 0), stop=(cb == CB - 1))
+            nc.tensor.matmul(mean[:], averager[:], total[:], start=True, stop=True)
             xc = norm.tile([P, CB, T], F32, name="xc")
             var = stat_ps.tile([P, T], F32, name="var", tag="stat")
             for cb in range(CB):
                 nc.vector.tensor_tensor(xc[:, cb, :], x[:, cb, cols], mean[:], ALU.subtract)
                 sq = norm.tile([P, T], BF16, name="sq", bufs=4)
-                nc.vector.tensor_tensor(sq[:], xc[:, cb, :], xc[:, cb, :], ALU.mult)
+                nc.scalar.square(sq[:], xc[:, cb, :])
                 nc.tensor.matmul(var[:], averager[:], sq[:], start=(cb == 0), stop=(cb == CB - 1))
-            logv = norm.tile([P, T], F32, name="logv")
-            nc.scalar.activation(logv[:], var[:], FN.Ln, bias=eps[:, 0:1])
             rstd = norm.tile([P, T], F32, name="rstd")
-            nc.scalar.activation(rstd[:], logv[:], FN.Exp, scale=-0.5)
+            nc.scalar.activation(rstd[:], var[:], FN.Abs_reciprocal_sqrt, bias=eps[:, 0:1])
             n = norm.tile([P, CB, T], BF16, name="n")
             for cb in range(CB):
                 gain = ln_cols[:, v * CB + cb : v * CB + cb + 1]

@@ -121,7 +121,7 @@ def tile_tinygpt_ntp_b_kernel(
             return n
 
         n1 = [layer_norm(h0, s, 0) for s in range(B)]
-        n2 = []
+        o = [late.tile([P, H, T], BF16, name=f"o{s}") for s in range(B)]
 
         with ExitStack() as attention_pools:
             soft = attention_pools.enter_context(tc.tile_pool(name="soft", bufs=3))
@@ -187,21 +187,19 @@ def tile_tinygpt_ntp_b_kernel(
                     )
                 return p_t
 
-            def weighted_values(head, v_t, p_t, o):
+            def weighted_values(s, head, v_t, p_t):
                 o_ps = att_ps.tile([P, T], F32, name="o_ps")
                 for ib in range(TB):
                     nc.tensor.matmul(
                         o_ps[:, ib * P : T], v_t[:, ib, head * DH : (head + 1) * DH], p_t[:, ib, ib * P : T],
                         start=(ib == 0), stop=(ib == TB - 1),
                     )
-                nc.scalar.copy(o[:, head, :], o_ps[:])
+                nc.scalar.copy(o[s][:, head, :], o_ps[:])
 
             for s in range(B):
-                cols = slice(s * T, (s + 1) * T)
                 q = late.tile([P, H, T], BF16, name=f"q{s}")
                 k = late.tile([P, H, T], BF16, name=f"k{s}")
                 v_t = late.tile([P, TB, C], BF16, name=f"v_t{s}")
-                o = late.tile([P, H, T], BF16, name=f"o{s}")
                 project_qk(s, 0, q, k)
                 for head in range(H):
                     p_t = softmax_weights(head, q, k)
@@ -209,17 +207,20 @@ def tile_tinygpt_ntp_b_kernel(
                         project_v(s, v_t)
                     if head + 1 < H:
                         project_qk(s, head + 1, q, k)
-                    weighted_values(head, v_t, p_t, o)
+                    weighted_values(s, head, v_t, p_t)
 
-                for cb in range(CB):
-                    h_ps = stat_ps.tile([P, T], F32, name="h_ps", tag="stat")
-                    for head in range(H):
-                        nc.tensor.matmul(
-                            h_ps[:], proj_sb[:, head, cb * P : (cb + 1) * P], o[:, head, :],
-                            start=(head == 0), stop=(head == H - 1),
-                        )
-                    nc.vector.tensor_tensor(h1[:, cb, cols], h0[:, cb, cols], h_ps[:], ALU.add)
-                n2.append(layer_norm(h1, s, 2))
+        n2 = []
+        for s in range(B):
+            cols = slice(s * T, (s + 1) * T)
+            for cb in range(CB):
+                h_ps = stat_ps.tile([P, T], F32, name="h_ps", tag="stat")
+                for head in range(H):
+                    nc.tensor.matmul(
+                        h_ps[:], proj_sb[:, head, cb * P : (cb + 1) * P], o[s][:, head, :],
+                        start=(head == 0), stop=(head == H - 1),
+                    )
+                nc.vector.tensor_tensor(h1[:, cb, cols], h0[:, cb, cols], h_ps[:], ALU.add)
+            n2.append(layer_norm(h1, s, 2))
 
         with tc.psum_pool(name="mlp_ps", bufs=6) as mlp_ps:
             for s in range(B):

@@ -175,9 +175,7 @@ def tile_tinygpt_ntp_b_kernel(
                     inv_sum = soft.tile([P, 1], F32, name="inv_sum")
                     nc.vector.reciprocal(inv_sum[:], e_sum[:])
                     p = soft.tile([P, T], BF16, name="p")
-                    nc.gpsimd.tensor_scalar(
-                        p[:, 0:width], e[:, 0:width], inv_sum[:, 0:1], 1.0, op0=ALU.mult, op1=ALU.mult
-                    )
+                    nc.vector.tensor_scalar_mul(p[:, 0:width], e[:, 0:width], inv_sum[:, 0:1])
                     pt_ps = att_ps.tile([P, T], BF16, name="pt_ps")
                     for ib in range(jb + 1):
                         nc.tensor.transpose(pt_ps[:, ib * P : (ib + 1) * P], p[:, ib * P : (ib + 1) * P], ident[:])

@@ -115,7 +115,7 @@ def tile_tinygpt_ntp_b_kernel(
                 xn = norm.tile([P, T], F32, name="xn", bufs=4)
                 nc.vector.tensor_tensor(xn[:], xc[:, cb, :], rstd[:], ALU.mult)
                 if cb % 2 == 0:
-                    nc.gpsimd.tensor_scalar(n[:, cb, :], xn[:], gain, bias, op0=ALU.mult, op1=ALU.add)
+                    nc.vector.tensor_scalar(n[:, cb, :], xn[:], gain, bias, op0=ALU.mult, op1=ALU.add)
                 else:
                     nc.scalar.activation(n[:, cb, :], xn[:], FN.Identity, bias=bias, scale=gain)
             return n

@@ -123,6 +123,25 @@ def tile_tinygpt_ntp_b_kernel(
         n1 = [layer_norm(h0, s, 0) for s in range(B)]
         o = [late.tile([P, H, T], BF16, name=f"o{s}") for s in range(B)]
 
+        def attention_output(s):
+            cols = slice(s * T, (s + 1) * T)
+            for cb in range(CB):
+                h_ps = stat_ps.tile([P, T], F32, name="h_ps", tag="stat")
+                for head in range(H):
+                    nc.tensor.matmul(
+                        h_ps[:], proj_sb[:, head, cb * P : (cb + 1) * P], o[s][:, head, :],
+                        start=(head == 0), stop=(head == H - 1),
+                    )
+                nc.vector.tensor_tensor(h1[:, cb, cols], h0[:, cb, cols], h_ps[:], ALU.add)
+            return layer_norm(h1, s, 2)
+
+        def hidden_sums(u_ps, n2, fb):
+            for cb in range(CB):
+                nc.tensor.matmul(
+                    u_ps[:], fc1_sb[:, cb, fb * P : (fb + 1) * P], n2[:, cb, :],
+                    start=(cb == 0), stop=(cb == CB - 1),
+                )
+
         with ExitStack() as attention_pools:
             soft = attention_pools.enter_context(tc.tile_pool(name="soft", bufs=3))
             qkv_ps = attention_pools.enter_context(tc.psum_pool(name="qkv_ps", bufs=2))
@@ -206,32 +225,24 @@ def tile_tinygpt_ntp_b_kernel(
                     if head + 1 < H:
                         project_qk(s, head + 1, q, k)
                     weighted_values(s, head, v_t, p_t)
+                if s == 0:
+                    n2_first = attention_output(0)
 
-        n2 = []
-        for s in range(B):
-            cols = slice(s * T, (s + 1) * T)
-            for cb in range(CB):
-                h_ps = stat_ps.tile([P, T], F32, name="h_ps", tag="stat")
-                for head in range(H):
-                    nc.tensor.matmul(
-                        h_ps[:], proj_sb[:, head, cb * P : (cb + 1) * P], o[s][:, head, :],
-                        start=(head == 0), stop=(head == H - 1),
-                    )
-                nc.vector.tensor_tensor(h1[:, cb, cols], h0[:, cb, cols], h_ps[:], ALU.add)
-            n2.append(layer_norm(h1, s, 2))
+            parked = late.tile([P, FB, T], F32, name="parked")
+            for fb in range(FB):
+                u_ps = qkv_ps.tile([P, T], F32, name="u_ps", tag="qkv")
+                hidden_sums(u_ps, n2_first, fb)
+                if fb % 2 == 0:
+                    nc.vector.tensor_copy(parked[:, fb, :], u_ps[:])
+                else:
+                    nc.scalar.copy(parked[:, fb, :], u_ps[:])
 
-        with tc.psum_pool(name="mlp_ps", bufs=6) as mlp_ps:
-            for s in range(B):
+        n2_second = attention_output(1)
+
+        with tc.tile_pool(name="hidden", bufs=1) as hidden, tc.psum_pool(name="mlp_ps", bufs=6) as mlp_ps:
+
+            def mlp_output(s, u):
                 cols = slice(s * T, (s + 1) * T)
-                u = late.tile([P, FB, T], BF16, name=f"u{s}")
-                for fb in range(FB):
-                    u_ps = mlp_ps.tile([P, T], F32, name="u_ps", tag="mlp")
-                    for cb in range(CB):
-                        nc.tensor.matmul(
-                            u_ps[:], fc1_sb[:, cb, fb * P : (fb + 1) * P], n2[s][:, cb, :],
-                            start=(cb == 0), stop=(cb == CB - 1),
-                        )
-                    nc.scalar.activation(u[:, fb, :], u_ps[:], FN.Gelu)
                 for cb in range(CB):
                     y_ps = mlp_ps.tile([P, T], F32, name="y_ps", tag="mlp")
                     for fb in range(FB):
@@ -242,3 +253,15 @@ def tile_tinygpt_ntp_b_kernel(
                     y = late.tile([P, T], F32, name="y", bufs=3)
                     nc.vector.tensor_tensor(y[:], h1[:, cb, cols], y_ps[:], ALU.add)
                     nc.sync.dma_start(out[cb * P : (cb + 1) * P, cols], y[:])
+
+            u_first = hidden.tile([P, FB, T], BF16, name="u_first")
+            for fb in range(FB):
+                nc.scalar.activation(u_first[:, fb, :], parked[:, fb, :], FN.Gelu)
+            mlp_output(0, u_first)
+
+            u_second = hidden.tile([P, FB, T], BF16, name="u_second")
+            for fb in range(FB):
+                u_ps = mlp_ps.tile([P, T], F32, name="u_ps", tag="mlp")
+                hidden_sums(u_ps, n2_second, fb)
+                nc.scalar.activation(u_second[:, fb, :], u_ps[:], FN.Gelu)
+            mlp_output(1, u_second)

@@ -1,4 +1,3 @@
-import math
 from contextlib import ExitStack
 
 import concourse.mybir as mybir
@@ -18,6 +17,7 @@ CB = C // P
 FB = F // P
 TB = T // P
 EPS = 1e-5
+HALF = T // 2
 MASKED = -1e30
 
 FLOPS = 2 * N * C * E + 4 * B * H * DH * (T * (T + 1) // 2) + 2 * N * C * C + 4 * N * C * F
@@ -31,6 +31,7 @@ def tile_tinygpt_ntp_b_kernel(
         held = pools.enter_context(tc.tile_pool(name="held", bufs=1))
         norm = pools.enter_context(tc.tile_pool(name="norm", bufs=2))
         stat_ps = pools.enter_context(tc.psum_pool(name="stat_ps", bufs=2))
+        qkv_ps = pools.enter_context(tc.psum_pool(name="qkv_ps", bufs=2))
 
         offsets = held.tile([P, N // 16], U16, name="offsets")
         nc.sync.dma_start(offsets[:], offs)
@@ -56,7 +57,38 @@ def tile_tinygpt_ntp_b_kernel(
         proj_sb = held.tile([P, CB, C], BF16, name="proj_sb")
         fc1_sb = held.tile([P, CB, F], BF16, name="fc1_sb")
         fc2_sb = held.tile([P, FB, C], BF16, name="fc2_sb")
-        with tc.tile_pool(name="table", bufs=1) as table:
+
+        def layer_norm(x, n, s, first, width, v, banks):
+            here = slice(first, first + width)
+            cols = slice(s * T + first, s * T + first + width)
+            part = norm.tile([P, width], F32, name="part")
+            nc.vector.tensor_tensor(part[:], x[:, 0, cols], x[:, 1, cols], ALU.add)
+            nc.vector.tensor_tensor(part[:], part[:], x[:, 2, cols], ALU.add)
+            total = norm.tile([P, width], BF16, name="total")
+            nc.vector.tensor_tensor(total[:], part[:], x[:, 3, cols], ALU.add)
+            mean = banks.tile([P, width], F32, name="mean", tag="stat")
+            nc.tensor.matmul(mean[:], averager[:], total[:], start=True, stop=True)
+            xc = norm.tile([P, CB, width], F32, name="xc")
+            var = banks.tile([P, width], F32, name="var", tag="stat")
+            for cb in range(CB):
+                nc.vector.tensor_tensor(xc[:, cb, :], x[:, cb, cols], mean[:], ALU.subtract)
+                sq = norm.tile([P, width], BF16, name="sq", bufs=4)
+                nc.scalar.square(sq[:], xc[:, cb, :])
+                nc.tensor.matmul(var[:], averager[:], sq[:], start=(cb == 0), stop=(cb == CB - 1))
+            rstd = norm.tile([P, width], F32, name="rstd")
+            nc.scalar.activation(rstd[:], var[:], FN.Abs_reciprocal_sqrt, bias=eps[:, 0:1])
+            for cb in range(CB):
+                gain = ln_cols[:, v * CB + cb : v * CB + cb + 1]
+                bias = ln_cols[:, (v + 1) * CB + cb : (v + 1) * CB + cb + 1]
+                xn = norm.tile([P, width], F32, name="xn", bufs=4)
+                nc.vector.tensor_tensor(xn[:], xc[:, cb, :], rstd[:], ALU.mult)
+                if cb % 2 == 0:
+                    nc.vector.tensor_scalar(n[:, cb, here], xn[:], gain, bias, op0=ALU.mult, op1=ALU.add)
+                else:
+                    nc.scalar.activation(n[:, cb, here], xn[:], FN.Identity, bias=bias, scale=gain)
+
+        n1 = [norm.tile([P, CB, T], BF16, name="n") for s in range(B)]
+        with tc.tile_pool(name="table", bufs=1) as table, tc.psum_pool(name="first_ps", bufs=4) as first_ps:
             pos_sb = table.tile([P, CB, T], F32, name="pos_sb")
             nc.scalar.dma_start(pos_sb[:], pos_emb.rearrange("(cb p) t -> p cb t", p=P))
             tok = []
@@ -73,54 +105,24 @@ def tile_tinygpt_ntp_b_kernel(
                 nc.scalar.dma_start(
                     ln_rows[v * CB : (v + 1) * CB, :], vec.rearrange("(cb p) o -> cb (p o)", p=P)
                 )
-            for s in range(B):
+            ln_ps = stat_ps.tile([P, T], F32, name="ln_ps", tag="stat")
+            nc.tensor.transpose(ln_ps[:, 0:64], ln_rows[:], ident64[:])
+            ln_cols = held.tile([P, 4 * CB], F32, name="ln_cols")
+            nc.vector.tensor_copy(ln_cols[:], ln_ps[:, 0 : 4 * CB])
+
+            for first in range(0, N, HALF):
                 for cb in range(CB):
                     nc.vector.tensor_tensor(
-                        h0[:, cb, s * T : (s + 1) * T],
-                        tok[cb][:].indirect(offsets[:, s * (T // 16) : (s + 1) * (T // 16)]),
-                        pos_sb[:, cb, :],
+                        h0[:, cb, first : first + HALF],
+                        tok[cb][:].indirect(offsets[:, first // 16 : (first + HALF) // 16]),
+                        pos_sb[:, cb, first % T : first % T + HALF],
                         ALU.add,
                     )
-
-        ln_ps = stat_ps.tile([P, T], F32, name="ln_ps", tag="stat")
-        nc.tensor.transpose(ln_ps[:, 0:64], ln_rows[:], ident64[:])
-        ln_cols = held.tile([P, 4 * CB], F32, name="ln_cols")
-        nc.vector.tensor_copy(ln_cols[:], ln_ps[:, 0 : 4 * CB])
+                layer_norm(h0, n1[first // T], first // T, first % T, HALF, 0, first_ps)
 
         late = pools.enter_context(tc.tile_pool(name="late", bufs=1))
         h1 = late.tile([P, CB, N], F32, name="h1")
 
-        def layer_norm(x, s, v):
-            cols = slice(s * T, (s + 1) * T)
-            part = norm.tile([P, T], F32, name="part")
-            nc.vector.tensor_tensor(part[:], x[:, 0, cols], x[:, 1, cols], ALU.add)
-            nc.vector.tensor_tensor(part[:], part[:], x[:, 2, cols], ALU.add)
-            total = norm.tile([P, T], BF16, name="total")
-            nc.vector.tensor_tensor(total[:], part[:], x[:, 3, cols], ALU.add)
-            mean = stat_ps.tile([P, T], F32, name="mean", tag="stat")
-            nc.tensor.matmul(mean[:], averager[:], total[:], start=True, stop=True)
-            xc = norm.tile([P, CB, T], F32, name="xc")
-            var = stat_ps.tile([P, T], F32, name="var", tag="stat")
-            for cb in range(CB):
-                nc.vector.tensor_tensor(xc[:, cb, :], x[:, cb, cols], mean[:], ALU.subtract)
-                sq = norm.tile([P, T], BF16, name="sq", bufs=4)
-                nc.scalar.square(sq[:], xc[:, cb, :])
-                nc.tensor.matmul(var[:], averager[:], sq[:], start=(cb == 0), stop=(cb == CB - 1))
-            rstd = norm.tile([P, T], F32, name="rstd")
-            nc.scalar.activation(rstd[:], var[:], FN.Abs_reciprocal_sqrt, bias=eps[:, 0:1])
-            n = norm.tile([P, CB, T], BF16, name="n")
-            for cb in range(CB):
-                gain = ln_cols[:, v * CB + cb : v * CB + cb + 1]
-                bias = ln_cols[:, (v + 1) * CB + cb : (v + 1) * CB + cb + 1]
-                xn = norm.tile([P, T], F32, name="xn", bufs=4)
-                nc.vector.tensor_tensor(xn[:], xc[:, cb, :], rstd[:], ALU.mult)
-                if cb % 2 == 0:
-                    nc.vector.tensor_scalar(n[:, cb, :], xn[:], gain, bias, op0=ALU.mult, op1=ALU.add)
-                else:
-                    nc.scalar.activation(n[:, cb, :], xn[:], FN.Identity, bias=bias, scale=gain)
-            return n
-
-        n1 = [layer_norm(h0, s, 0) for s in range(B)]
         o = [late.tile([P, H, T], BF16, name=f"o{s}") for s in range(B)]
 
         def attention_output(s):
@@ -133,7 +135,9 @@ def tile_tinygpt_ntp_b_kernel(
                         start=(head == 0), stop=(head == H - 1),
                     )
                 nc.vector.tensor_tensor(h1[:, cb, cols], h0[:, cb, cols], h_ps[:], ALU.add)
-            return layer_norm(h1, s, 2)
+            n2 = norm.tile([P, CB, T], BF16, name="n")
+            layer_norm(h1, n2, s, 0, T, 2, stat_ps)
+            return n2
 
         def hidden_sums(u_ps, n2, fb):
             for cb in range(CB):
@@ -144,24 +148,20 @@ def tile_tinygpt_ntp_b_kernel(
 
         with ExitStack() as attention_pools:
             soft = attention_pools.enter_context(tc.tile_pool(name="soft", bufs=3))
-            qkv_ps = attention_pools.enter_context(tc.psum_pool(name="qkv_ps", bufs=2))
             att_ps = attention_pools.enter_context(tc.psum_pool(name="att_ps", bufs=1))
 
-            def project_qk(s, head, q, k):
-                q_ps = qkv_ps.tile([P, T], F32, name="q_ps", tag="qkv")
-                for cb in range(CB):
-                    nc.tensor.matmul(
-                        q_ps[:], qkv_sb[:, cb, head * DH : (head + 1) * DH], n1[s][:, cb, :],
-                        start=(cb == 0), stop=(cb == CB - 1),
-                    )
-                nc.scalar.mul(q[:, head, :], q_ps[:], 1.0 / math.sqrt(DH))
-                k_ps = qkv_ps.tile([P, T], F32, name="k_ps", tag="qkv")
-                for cb in range(CB):
-                    nc.tensor.matmul(
-                        k_ps[:], qkv_sb[:, cb, C + head * DH : C + (head + 1) * DH], n1[s][:, cb, :],
-                        start=(cb == 0), stop=(cb == CB - 1),
-                    )
-                nc.scalar.copy(k[:, head, :], k_ps[:])
+            def project_qk(s, head, qk):
+                for first in range(0, T, HALF):
+                    half = slice(first, first + HALF)
+                    qk_ps = qkv_ps.tile([P, 2, HALF], F32, name="qk_ps", tag="qkv")
+                    for which in range(2):
+                        row0 = which * C + head * DH
+                        for cb in range(CB):
+                            nc.tensor.matmul(
+                                qk_ps[:, which, :], qkv_sb[:, cb, row0 : row0 + DH], n1[s][:, cb, half],
+                                start=(cb == 0), stop=(cb == CB - 1),
+                            )
+                    nc.scalar.mul(qk[:, :, head, half], qk_ps[:], DH ** -0.25)
 
             def project_v(s, v_t):
                 for tb in range(TB):
@@ -173,17 +173,17 @@ def tile_tinygpt_ntp_b_kernel(
                         )
                     nc.scalar.copy(v_t[:, tb, :], v_ps[:])
 
-            def softmax_weights(head, q, k):
+            def softmax_weights(head, qk):
                 p_t = soft.tile([P, TB, T], BF16, name="p_t", bufs=2)
                 for jb in range(TB):
                     seen = jb * P
                     width = seen + P
-                    q_blk = q[:, head, seen:width]
+                    q_blk = qk[:, 0, head, seen:width]
                     sc = att_ps.tile([P, T], F32, name="sc", bufs=2)
                     if jb > 0:
-                        nc.tensor.matmul(sc[:, 0:seen], q_blk, k[:, head, 0:seen], start=True, stop=True)
+                        nc.tensor.matmul(sc[:, 0:seen], q_blk, qk[:, 1, head, 0:seen], start=True, stop=True)
                     nc.tensor.matmul(sc[:, seen:width], ident[:], causal[:], start=True, stop=False)
-                    nc.tensor.matmul(sc[:, seen:width], q_blk, k[:, head, seen:width], start=False, stop=True)
+                    nc.tensor.matmul(sc[:, seen:width], q_blk, qk[:, 1, head, seen:width], start=False, stop=True)
                     neg_max = soft.tile([P, 1], F32, name="neg_max")
                     nc.vector.reduce_max(neg_max[:], sc[:, 0:width], axis=AXIS_X, negate=True)
                     e = soft.tile([P, T], F32, name="e")
@@ -214,16 +214,15 @@ def tile_tinygpt_ntp_b_kernel(
                 nc.scalar.copy(o[s][:, head, :], o_ps[:])
 
             for s in range(B):
-                q = late.tile([P, H, T], BF16, name=f"q{s}")
-                k = late.tile([P, H, T], BF16, name=f"k{s}")
+                qk = late.tile([P, 2, H, T], BF16, name=f"qk{s}")
                 v_t = late.tile([P, TB, C], BF16, name=f"v_t{s}")
-                project_qk(s, 0, q, k)
+                project_qk(s, 0, qk)
                 for head in range(H):
-                    p_t = softmax_weights(head, q, k)
+                    p_t = softmax_weights(head, qk)
                     if head == 0:
                         project_v(s, v_t)
                     if head + 1 < H:
-                        project_qk(s, head + 1, q, k)
+                        project_qk(s, head + 1, qk)
                     weighted_values(s, head, v_t, p_t)
                 if s == 0:
                     n2_first = attention_output(0)
@@ -239,7 +238,7 @@ def tile_tinygpt_ntp_b_kernel(
 
         n2_second = attention_output(1)
 
-        with tc.tile_pool(name="hidden", bufs=1) as hidden, tc.psum_pool(name="mlp_ps", bufs=6) as mlp_ps:
+        with tc.tile_pool(name="hidden", bufs=1) as hidden, tc.psum_pool(name="mlp_ps", bufs=4) as mlp_ps:
 
             def mlp_output(s, u):
                 cols = slice(s * T, (s + 1) * T)

@@ -110,15 +110,15 @@ def tile_tinygpt_ntp_b_kernel(
             ln_cols = held.tile([P, 4 * CB], F32, name="ln_cols")
             nc.vector.tensor_copy(ln_cols[:], ln_ps[:, 0 : 4 * CB])
 
-            for first in range(0, N, HALF):
+            for first, width in ((0, HALF), (HALF, HALF), (T, T)):
                 for cb in range(CB):
                     nc.vector.tensor_tensor(
-                        h0[:, cb, first : first + HALF],
-                        tok[cb][:].indirect(offsets[:, first // 16 : (first + HALF) // 16]),
-                        pos_sb[:, cb, first % T : first % T + HALF],
+                        h0[:, cb, first : first + width],
+                        tok[cb][:].indirect(offsets[:, first // 16 : (first + width) // 16]),
+                        pos_sb[:, cb, first % T : first % T + width],
                         ALU.add,
                     )
-                layer_norm(h0, n1[first // T], first // T, first % T, HALF, 0, first_ps)
+                layer_norm(h0, n1[first // T], first // T, first % T, width, 0, first_ps)
 
         late = pools.enter_context(tc.tile_pool(name="late", bufs=1))
         h1 = late.tile([P, CB, N], F32, name="h1")

@@ -1,4 +1,5 @@
 from contextlib import ExitStack
+from functools import partial
 
 import concourse.mybir as mybir
 from concourse.masks import make_identity
@@ -46,6 +47,12 @@ def tile_tinygpt_ntp_b_kernel(
         nc.vector.tensor_scalar(causal[:], ahead[:], 0.0, MASKED, op0=ALU.is_gt, op1=ALU.mult)
         averager = held.tile([P, P], BF16, name="averager")
         nc.vector.memset(averager[:], 1.0 / C)
+        mean_column = held.tile([P, 1], BF16, name="mean_column")
+        nc.vector.memset(mean_column[:], 1.0 / C)
+        ident_f32 = held.tile([P, P], F32, name="ident_f32")
+        make_identity(nc, ident_f32[:])
+        minus_half = held.tile([P, TB], F32, name="minus_half")
+        nc.vector.memset(minus_half[:], -0.5)
         eps = held.tile([P, 1], F32, name="eps")
         nc.vector.memset(eps[:], EPS)
         warm = held.tile([P, 1], F32, name="warm")
@@ -58,7 +65,28 @@ def tile_tinygpt_ntp_b_kernel(
         fc1_sb = held.tile([P, CB, F], BF16, name="fc1_sb")
         fc2_sb = held.tile([P, FB, C], BF16, name="fc2_sb")
 
-        def layer_norm(x, n, s, first, width, v, banks):
+        def rstd_by_power(squares, width, banks):
+            blocks = width // P
+            var = banks.tile([P, TB], F32, name="var_columns", tag="stat")
+            for jb in range(blocks):
+                for cb in range(CB):
+                    nc.tensor.matmul(
+                        var[:, jb : jb + 1], squares[cb][:, jb * P : (jb + 1) * P], mean_column[:],
+                        start=(cb == 0), stop=(cb == CB - 1),
+                    )
+            var_eps = norm.tile([P, TB], F32, name="var_eps")
+            nc.vector.tensor_scalar_add(var_eps[:, 0:blocks], var[:, 0:blocks], EPS)
+            column = norm.tile([P, TB], F32, name="column")
+            nc.gpsimd.tensor_tensor(column[:, 0:blocks], var_eps[:, 0:blocks], minus_half[:, 0:blocks], ALU.pow)
+            rstd = banks.tile([P, T], F32, name="rstd_rows", tag="stat")
+            for jb in range(blocks):
+                nc.tensor.matmul(
+                    rstd[:, jb * P : (jb + 1) * P], column[:, jb : jb + 1].to_broadcast([P, P]), ident_f32[:],
+                    start=True, stop=True,
+                )
+            return rstd
+
+        def layer_norm(x, n, s, first, width, v, banks, by_power=False):
             here = slice(first, first + width)
             cols = slice(s * T + first, s * T + first + width)
             part = norm.tile([P, width], F32, name="part")
@@ -69,25 +97,31 @@ def tile_tinygpt_ntp_b_kernel(
             mean = banks.tile([P, width], F32, name="mean", tag="stat")
             nc.tensor.matmul(mean[:], averager[:], total[:], start=True, stop=True)
             xc = norm.tile([P, CB, width], F32, name="xc")
-            var = banks.tile([P, width], F32, name="var", tag="stat")
+            squares = []
             for cb in range(CB):
                 nc.vector.tensor_tensor(xc[:, cb, :], x[:, cb, cols], mean[:], ALU.subtract)
-                sq = norm.tile([P, width], BF16, name="sq", bufs=4)
+                sq = norm.tile([P, width], BF16, name="sq", bufs=CB)
                 nc.scalar.square(sq[:], xc[:, cb, :])
-                nc.tensor.matmul(var[:], averager[:], sq[:], start=(cb == 0), stop=(cb == CB - 1))
-            rstd = norm.tile([P, width], F32, name="rstd")
-            nc.scalar.activation(rstd[:], var[:], FN.Abs_reciprocal_sqrt, bias=eps[:, 0:1])
+                squares.append(sq)
+            if by_power:
+                rstd = rstd_by_power(squares, width, banks)
+            else:
+                var = banks.tile([P, width], F32, name="var", tag="stat")
+                for cb in range(CB):
+                    nc.tensor.matmul(var[:], averager[:], squares[cb][:], start=(cb == 0), stop=(cb == CB - 1))
+                rstd = norm.tile([P, width], F32, name="rstd")
+                nc.scalar.activation(rstd[:], var[:], FN.Abs_reciprocal_sqrt, bias=eps[:, 0:1])
             for cb in range(CB):
                 gain = ln_cols[:, v * CB + cb : v * CB + cb + 1]
                 bias = ln_cols[:, (v + 1) * CB + cb : (v + 1) * CB + cb + 1]
                 xn = norm.tile([P, width], F32, name="xn", bufs=4)
-                nc.vector.tensor_tensor(xn[:], xc[:, cb, :], rstd[:], ALU.mult)
+                nc.vector.tensor_tensor(xn[:], xc[:, cb, :], rstd[:, 0:width], ALU.mult)
                 if cb % 2 == 0:
                     nc.vector.tensor_scalar(n[:, cb, here], xn[:], gain, bias, op0=ALU.mult, op1=ALU.add)
                 else:
                     nc.scalar.activation(n[:, cb, here], xn[:], FN.Identity, bias=bias, scale=gain)
 
-        n1 = [norm.tile([P, CB, T], BF16, name="n") for s in range(B)]
+        n1 = [held.tile([P, CB, T], BF16, name=f"n1_{s}") for s in range(B)]
         with tc.tile_pool(name="table", bufs=1) as table, tc.psum_pool(name="first_ps", bufs=4) as first_ps:
             pos_sb = table.tile([P, CB, T], F32, name="pos_sb")
             nc.scalar.dma_start(pos_sb[:], pos_emb.rearrange("(cb p) t -> p cb t", p=P))
@@ -118,31 +152,31 @@ def tile_tinygpt_ntp_b_kernel(
                         pos_sb[:, cb, first % T : first % T + width],
                         ALU.add,
                     )
-                layer_norm(h0, n1[first // T], first // T, first % T, width, 0, first_ps)
+                if first < T:
+                    layer_norm(h0, n1[0], 0, first, width, 0, first_ps)
 
         late = pools.enter_context(tc.tile_pool(name="late", bufs=1))
         h1 = late.tile([P, CB, N], F32, name="h1")
-
+        qk = [late.tile([P, 2, H, T], BF16, name=f"qk{s}") for s in range(B)]
+        v_t = [late.tile([P, TB, C], BF16, name=f"v_t{s}") for s in range(B)]
         o = [late.tile([P, H, T], BF16, name=f"o{s}") for s in range(B)]
+        n2 = [late.tile([P, CB, T], BF16, name=f"n2_{s}") for s in range(B)]
+        parked = late.tile([P, FB, T], F32, name="parked")
 
-        def attention_output(s):
+        def project_out(s, cb):
             cols = slice(s * T, (s + 1) * T)
-            for cb in range(CB):
-                h_ps = stat_ps.tile([P, T], F32, name="h_ps", tag="stat")
-                for head in range(H):
-                    nc.tensor.matmul(
-                        h_ps[:], proj_sb[:, head, cb * P : (cb + 1) * P], o[s][:, head, :],
-                        start=(head == 0), stop=(head == H - 1),
-                    )
-                nc.vector.tensor_tensor(h1[:, cb, cols], h0[:, cb, cols], h_ps[:], ALU.add)
-            n2 = norm.tile([P, CB, T], BF16, name="n")
-            layer_norm(h1, n2, s, 0, T, 2, stat_ps)
-            return n2
+            h_ps = stat_ps.tile([P, T], F32, name="h_ps", tag="stat")
+            for head in range(H):
+                nc.tensor.matmul(
+                    h_ps[:], proj_sb[:, head, cb * P : (cb + 1) * P], o[s][:, head, :],
+                    start=(head == 0), stop=(head == H - 1),
+                )
+            nc.vector.tensor_tensor(h1[:, cb, cols], h0[:, cb, cols], h_ps[:], ALU.add)
 
-        def hidden_sums(u_ps, n2, fb):
+        def hidden_sums(u_ps, s, fb):
             for cb in range(CB):
                 nc.tensor.matmul(
-                    u_ps[:], fc1_sb[:, cb, fb * P : (fb + 1) * P], n2[:, cb, :],
+                    u_ps[:], fc1_sb[:, cb, fb * P : (fb + 1) * P], n2[s][:, cb, :],
                     start=(cb == 0), stop=(cb == CB - 1),
                 )
 
@@ -150,98 +184,123 @@ def tile_tinygpt_ntp_b_kernel(
             soft = attention_pools.enter_context(tc.tile_pool(name="soft", bufs=3))
             att_ps = attention_pools.enter_context(tc.psum_pool(name="att_ps", bufs=1))
 
-            def project_qk(s, head, qk):
-                for first in range(0, T, HALF):
-                    half = slice(first, first + HALF)
-                    qk_ps = qkv_ps.tile([P, 2, HALF], F32, name="qk_ps", tag="qkv")
-                    for which in range(2):
-                        row0 = which * C + head * DH
-                        for cb in range(CB):
-                            nc.tensor.matmul(
-                                qk_ps[:, which, :], qkv_sb[:, cb, row0 : row0 + DH], n1[s][:, cb, half],
-                                start=(cb == 0), stop=(cb == CB - 1),
-                            )
-                    nc.scalar.mul(qk[:, :, head, half], qk_ps[:], DH ** -0.25)
-
-            def project_v(s, v_t):
-                for tb in range(TB):
-                    v_ps = qkv_ps.tile([P, C], F32, name="v_ps", tag="qkv")
+            def project_qk(s, head, first):
+                half = slice(first, first + HALF)
+                qk_ps = qkv_ps.tile([P, 2, HALF], F32, name="qk_ps", tag="qkv")
+                for which in range(2):
+                    row0 = which * C + head * DH
                     for cb in range(CB):
                         nc.tensor.matmul(
-                            v_ps[:], n1[s][:, cb, tb * P : (tb + 1) * P], qkv_sb[:, cb, 2 * C : 3 * C],
+                            qk_ps[:, which, :], qkv_sb[:, cb, row0 : row0 + DH], n1[s][:, cb, half],
                             start=(cb == 0), stop=(cb == CB - 1),
                         )
-                    nc.scalar.copy(v_t[:, tb, :], v_ps[:])
+                nc.scalar.mul(qk[s][:, :, head, half], qk_ps[:], DH ** -0.25)
 
-            def softmax_weights(head, qk):
-                p_t = soft.tile([P, TB, T], BF16, name="p_t", bufs=2)
-                for jb in range(TB):
-                    seen = jb * P
-                    width = seen + P
-                    q_blk = qk[:, 0, head, seen:width]
-                    sc = att_ps.tile([P, T], F32, name="sc", bufs=2)
-                    if jb > 0:
-                        nc.tensor.matmul(sc[:, 0:seen], q_blk, qk[:, 1, head, 0:seen], start=True, stop=True)
-                    nc.tensor.matmul(sc[:, seen:width], ident[:], causal[:], start=True, stop=False)
-                    nc.tensor.matmul(sc[:, seen:width], q_blk, qk[:, 1, head, seen:width], start=False, stop=True)
-                    neg_max = soft.tile([P, 1], F32, name="neg_max")
-                    nc.vector.reduce_max(neg_max[:], sc[:, 0:width], axis=AXIS_X, negate=True)
-                    e = soft.tile([P, T], F32, name="e")
-                    e_sum = soft.tile([P, 1], F32, name="e_sum")
-                    nc.scalar.activation(
-                        e[:, 0:width], sc[:, 0:width], FN.Exp, bias=neg_max[:, 0:1], accum_out=e_sum[:, 0:1]
-                    )
-                    inv_sum = soft.tile([P, 1], F32, name="inv_sum")
-                    nc.vector.reciprocal(inv_sum[:], e_sum[:])
-                    p = soft.tile([P, T], BF16, name="p")
-                    nc.vector.tensor_scalar_mul(p[:, 0:width], e[:, 0:width], inv_sum[:, 0:1])
-                    pt_ps = att_ps.tile([P, T], BF16, name="pt_ps")
-                    for ib in range(jb + 1):
-                        nc.tensor.transpose(pt_ps[:, ib * P : (ib + 1) * P], p[:, ib * P : (ib + 1) * P], ident[:])
-                    nc.vector.tensor_copy(
-                        p_t[:, 0 : jb + 1, seen:width],
-                        pt_ps[:, 0:width].rearrange("i (ib j) -> i ib j", j=P),
-                    )
-                return p_t
-
-            def weighted_values(s, head, v_t, p_t):
-                o_ps = att_ps.tile([P, T], F32, name="o_ps")
-                for ib in range(TB):
+            def project_v(s, tb):
+                v_ps = qkv_ps.tile([P, C], F32, name="v_ps", tag="qkv")
+                for cb in range(CB):
                     nc.tensor.matmul(
-                        o_ps[:, ib * P : T], v_t[:, ib, head * DH : (head + 1) * DH], p_t[:, ib, ib * P : T],
-                        start=(ib == 0), stop=(ib == TB - 1),
+                        v_ps[:], n1[s][:, cb, tb * P : (tb + 1) * P], qkv_sb[:, cb, 2 * C : 3 * C],
+                        start=(cb == 0), stop=(cb == CB - 1),
                     )
-                nc.scalar.copy(o[s][:, head, :], o_ps[:])
+                nc.scalar.copy(v_t[s][:, tb, :], v_ps[:])
 
-            for s in range(B):
-                qk = late.tile([P, 2, H, T], BF16, name=f"qk{s}")
-                v_t = late.tile([P, TB, C], BF16, name=f"v_t{s}")
-                project_qk(s, 0, qk)
-                for head in range(H):
-                    p_t = softmax_weights(head, qk)
-                    if head == 0:
-                        project_v(s, v_t)
-                    if head + 1 < H:
-                        project_qk(s, head + 1, qk)
-                    weighted_values(s, head, v_t, p_t)
-                if s == 0:
-                    n2_first = attention_output(0)
-
-            parked = late.tile([P, FB, T], F32, name="parked")
-            for fb in range(FB):
+            def park(fb):
                 u_ps = qkv_ps.tile([P, T], F32, name="u_ps", tag="qkv")
-                hidden_sums(u_ps, n2_first, fb)
+                hidden_sums(u_ps, 0, fb)
                 if fb % 2 == 0:
                     nc.vector.tensor_copy(parked[:, fb, :], u_ps[:])
                 else:
                     nc.scalar.copy(parked[:, fb, :], u_ps[:])
 
-        n2_second = attention_output(1)
+            def softmax_block(s, head, jb, p_t):
+                seen = jb * P
+                width = seen + P
+                q_blk = qk[s][:, 0, head, seen:width]
+                sc = att_ps.tile([P, T], F32, name="sc", bufs=2)
+                if jb > 0:
+                    nc.tensor.matmul(sc[:, 0:seen], q_blk, qk[s][:, 1, head, 0:seen], start=True, stop=True)
+                nc.tensor.matmul(sc[:, seen:width], ident[:], causal[:], start=True, stop=False)
+                nc.tensor.matmul(sc[:, seen:width], q_blk, qk[s][:, 1, head, seen:width], start=False, stop=True)
+                neg_max = soft.tile([P, 1], F32, name="neg_max")
+                nc.vector.reduce_max(neg_max[:], sc[:, 0:width], axis=AXIS_X, negate=True)
+                e = soft.tile([P, T], F32, name="e")
+                e_sum = soft.tile([P, 1], F32, name="e_sum")
+                nc.scalar.activation(
+                    e[:, 0:width], sc[:, 0:width], FN.Exp, bias=neg_max[:, 0:1], accum_out=e_sum[:, 0:1]
+                )
+                inv_sum = soft.tile([P, 1], F32, name="inv_sum")
+                nc.vector.reciprocal(inv_sum[:], e_sum[:])
+                p = soft.tile([P, T], BF16, name="p")
+                nc.vector.tensor_scalar_mul(p[:, 0:width], e[:, 0:width], inv_sum[:, 0:1])
+                pt_ps = att_ps.tile([P, T], BF16, name="pt_ps")
+                for ib in range(jb + 1):
+                    nc.tensor.transpose(pt_ps[:, ib * P : (ib + 1) * P], p[:, ib * P : (ib + 1) * P], ident[:])
+                nc.vector.tensor_copy(
+                    p_t[:, 0 : jb + 1, seen:width],
+                    pt_ps[:, 0:width].rearrange("i (ib j) -> i ib j", j=P),
+                )
+
+            def weighted_values(s, head, p_t):
+                o_ps = att_ps.tile([P, T], F32, name="o_ps")
+                for ib in range(TB):
+                    nc.tensor.matmul(
+                        o_ps[:, ib * P : T], v_t[s][:, ib, head * DH : (head + 1) * DH], p_t[:, ib, ib * P : T],
+                        start=(ib == 0), stop=(ib == TB - 1),
+                    )
+                nc.scalar.copy(o[s][:, head, :], o_ps[:])
+
+            def attention(s, pieces):
+                ready = None
+                for head in range(H):
+                    p_t = soft.tile([P, TB, T], BF16, name="p_t", bufs=2)
+                    for jb in range(TB):
+                        softmax_block(s, head, jb, p_t)
+                        block = head * TB + jb
+                        if block < len(pieces):
+                            pieces[block]()
+                        if ready is not None and jb == 2:
+                            weighted_values(s, *ready)
+                    ready = (head, p_t)
+                for piece in pieces[H * TB :]:
+                    piece()
+                weighted_values(s, *ready)
+
+            for first in (0, HALF):
+                project_qk(0, 0, first)
+            warm_exp = soft.tile([P, 1], F32, name="warm_exp", bufs=1)
+            nc.scalar.activation(warm_exp[:], qk[0][:, 0, 0, 0:1], FN.Exp)
+            own = [partial(project_qk, 0, 1, first) for first in (0, HALF)]
+            own += [partial(project_v, 0, tb) for tb in range(TB)]
+            own += [partial(project_qk, 0, head, first) for head in (2, 3) for first in (0, HALF)]
+            first_norm = [partial(layer_norm, h0, n1[1], 1, 0, T, 0, stat_ps, by_power=True)]
+            attention(0, own[:TB] + first_norm + own[TB:])
+
+            for cb in range(CB):
+                project_out(0, cb)
+                if cb % 2 == 0:
+                    for first in (0, HALF):
+                        project_qk(1, cb // 2, first)
+                else:
+                    for tb in (cb - 1, cb):
+                        project_v(1, tb)
+            layer_norm(h1, n2[0], 0, 0, T, 2, stat_ps, by_power=True)
+
+            rest = [partial(project_qk, 1, head, first) for head in (2, 3) for first in (0, HALF)]
+            attention(1, rest + [partial(park, fb) for fb in range(FB)])
+            for cb in range(CB):
+                project_out(1, cb)
+            layer_norm(h1, n2[1], 1, 0, T, 2, stat_ps)
 
         with tc.tile_pool(name="hidden", bufs=1) as hidden, tc.psum_pool(name="mlp_ps", bufs=4) as mlp_ps:
 
-            def mlp_output(s, u):
+            def store(s, cb, y_ps):
                 cols = slice(s * T, (s + 1) * T)
+                y = late.tile([P, T], F32, name="y", bufs=3)
+                nc.vector.tensor_tensor(y[:], h1[:, cb, cols], y_ps[:], ALU.add)
+                nc.sync.dma_start(out[cb * P : (cb + 1) * P, cols], y[:])
+
+            def mlp_output(s, u):
                 for cb in range(CB):
                     y_ps = mlp_ps.tile([P, T], F32, name="y_ps", tag="mlp")
                     for fb in range(FB):
@@ -249,9 +308,7 @@ def tile_tinygpt_ntp_b_kernel(
                             y_ps[:], fc2_sb[:, fb, cb * P : (cb + 1) * P], u[:, fb, :],
                             start=(fb == 0), stop=(fb == FB - 1),
                         )
-                    y = late.tile([P, T], F32, name="y", bufs=3)
-                    nc.vector.tensor_tensor(y[:], h1[:, cb, cols], y_ps[:], ALU.add)
-                    nc.sync.dma_start(out[cb * P : (cb + 1) * P, cols], y[:])
+                    store(s, cb, y_ps)
 
             u_first = hidden.tile([P, FB, T], BF16, name="u_first")
             for fb in range(FB):
@@ -261,6 +318,6 @@ def tile_tinygpt_ntp_b_kernel(
             u_second = hidden.tile([P, FB, T], BF16, name="u_second")
             for fb in range(FB):
                 u_ps = mlp_ps.tile([P, T], F32, name="u_ps", tag="mlp")
-                hidden_sums(u_ps, n2_second, fb)
+                hidden_sums(u_ps, 1, fb)
                 nc.scalar.activation(u_second[:, fb, :], u_ps[:], FN.Gelu)
             mlp_output(1, u_second)

@@ -144,16 +144,16 @@ def tile_tinygpt_ntp_b_kernel(
             ln_cols = held.tile([P, 4 * CB], F32, name="ln_cols")
             nc.vector.tensor_copy(ln_cols[:], ln_ps[:, 0 : 4 * CB])
 
-            for first, width in ((0, HALF), (HALF, HALF), (T, T)):
+            for first in range(0, N, HALF):
                 for cb in range(CB):
                     nc.vector.tensor_tensor(
-                        h0[:, cb, first : first + width],
-                        tok[cb][:].indirect(offsets[:, first // 16 : (first + width) // 16]),
-                        pos_sb[:, cb, first % T : first % T + width],
+                        h0[:, cb, first : first + HALF],
+                        tok[cb][:].indirect(offsets[:, first // 16 : (first + HALF) // 16]),
+                        pos_sb[:, cb, first % T : first % T + HALF],
                         ALU.add,
                     )
                 if first < T:
-                    layer_norm(h0, n1[0], 0, first, width, 0, first_ps)
+                    layer_norm(h0, n1[0], 0, first, HALF, 0, first_ps)
 
         late = pools.enter_context(tc.tile_pool(name="late", bufs=1))
         h1 = late.tile([P, CB, N], F32, name="h1")
@@ -181,7 +181,7 @@ def tile_tinygpt_ntp_b_kernel(
                 )
 
         with ExitStack() as attention_pools:
-            soft = attention_pools.enter_context(tc.tile_pool(name="soft", bufs=3))
+            soft = attention_pools.enter_context(tc.tile_pool(name="soft", bufs=4))
             att_ps = attention_pools.enter_context(tc.psum_pool(name="att_ps", bufs=1))
 
             def project_qk(s, head, first):
@@ -195,6 +195,15 @@ def tile_tinygpt_ntp_b_kernel(
                             start=(cb == 0), stop=(cb == CB - 1),
                         )
                 nc.scalar.mul(qk[s][:, :, head, half], qk_ps[:], DH ** -0.25)
+
+            def project_whole(s, head, which):
+                row0 = which * C + head * DH
+                qk_ps = qkv_ps.tile([P, T], F32, name="qk_ps", tag="qkv")
+                for cb in range(CB):
+                    nc.tensor.matmul(
+                        qk_ps[:], qkv_sb[:, cb, row0 : row0 + DH], n1[s][:, cb, :], start=(cb == 0), stop=(cb == CB - 1),
+                    )
+                nc.scalar.mul(qk[s][:, which, head, :], qk_ps[:], DH ** -0.25)
 
             def project_v(s, tb):
                 v_ps = qkv_ps.tile([P, C], F32, name="v_ps", tag="qkv")
@@ -217,7 +226,7 @@ def tile_tinygpt_ntp_b_kernel(
                 seen = jb * P
                 width = seen + P
                 q_blk = qk[s][:, 0, head, seen:width]
-                sc = att_ps.tile([P, T], F32, name="sc", bufs=2)
+                sc = att_ps.tile([P, T], F32, name="sc", bufs=3)
                 if jb > 0:
                     nc.tensor.matmul(sc[:, 0:seen], q_blk, qk[s][:, 1, head, 0:seen], start=True, stop=True)
                 nc.tensor.matmul(sc[:, seen:width], ident[:], causal[:], start=True, stop=False)
@@ -242,7 +251,7 @@ def tile_tinygpt_ntp_b_kernel(
                 )
 
             def weighted_values(s, head, p_t):
-                o_ps = att_ps.tile([P, T], F32, name="o_ps")
+                o_ps = stat_ps.tile([P, T], F32, name="o_ps", tag="stat")
                 for ib in range(TB):
                     nc.tensor.matmul(
                         o_ps[:, ib * P : T], v_t[s][:, ib, head * DH : (head + 1) * DH], p_t[:, ib, ib * P : T],
@@ -250,44 +259,48 @@ def tile_tinygpt_ntp_b_kernel(
                     )
                 nc.scalar.copy(o[s][:, head, :], o_ps[:])
 
-            def attention(s, pieces):
+            def attention(s, groups):
                 ready = None
                 for head in range(H):
                     p_t = soft.tile([P, TB, T], BF16, name="p_t", bufs=2)
                     for jb in range(TB):
                         softmax_block(s, head, jb, p_t)
                         block = head * TB + jb
-                        if block < len(pieces):
-                            pieces[block]()
-                        if ready is not None and jb == 2:
+                        if block < len(groups):
+                            for piece in groups[block]:
+                                piece()
+                        if ready is not None and jb == TB - 1:
                             weighted_values(s, *ready)
                     ready = (head, p_t)
-                for piece in pieces[H * TB :]:
-                    piece()
+                for group in groups[H * TB :]:
+                    for piece in group:
+                        piece()
                 weighted_values(s, *ready)
 
             for first in (0, HALF):
                 project_qk(0, 0, first)
             warm_exp = soft.tile([P, 1], F32, name="warm_exp", bufs=1)
             nc.scalar.activation(warm_exp[:], qk[0][:, 0, 0, 0:1], FN.Exp)
-            own = [partial(project_qk, 0, 1, first) for first in (0, HALF)]
+            own = [partial(project_whole, 0, 1, which) for which in (0, 1)]
             own += [partial(project_v, 0, tb) for tb in range(TB)]
-            own += [partial(project_qk, 0, head, first) for head in (2, 3) for first in (0, HALF)]
-            first_norm = [partial(layer_norm, h0, n1[1], 1, 0, T, 0, stat_ps, by_power=True)]
-            attention(0, own[:TB] + first_norm + own[TB:])
+            own += [partial(project_whole, 0, head, which) for head in (2, 3) for which in (0, 1)]
+            groups = [[piece] for piece in own]
+            groups[2] += [partial(layer_norm, h0, n1[1], 1, 0, T, 0, stat_ps, by_power=True)]
+            attention(0, groups)
 
             for cb in range(CB):
                 project_out(0, cb)
                 if cb % 2 == 0:
-                    for first in (0, HALF):
-                        project_qk(1, cb // 2, first)
+                    for which in range(2):
+                        project_whole(1, cb // 2, which)
                 else:
                     for tb in (cb - 1, cb):
                         project_v(1, tb)
             layer_norm(h1, n2[0], 0, 0, T, 2, stat_ps, by_power=True)
 
-            rest = [partial(project_qk, 1, head, first) for head in (2, 3) for first in (0, HALF)]
-            attention(1, rest + [partial(park, fb) for fb in range(FB)])
+            rest = [partial(project_whole, 1, head, which) for head in (2, 3) for which in (0, 1)]
+            rest += [partial(park, fb) for fb in range(FB)]
+            attention(1, [[piece] for piece in rest])
             for cb in range(CB):
                 project_out(1, cb)
             layer_norm(h1, n2[1], 1, 0, T, 2, stat_ps)
@@ -310,14 +323,21 @@ def tile_tinygpt_ntp_b_kernel(
                         )
                     store(s, cb, y_ps)
 
-            u_first = hidden.tile([P, FB, T], BF16, name="u_first")
+            sums = [mlp_ps.tile([P, T], F32, name=f"y_ps{cb}", tag="mlp") for cb in range(CB)]
             for fb in range(FB):
-                nc.scalar.activation(u_first[:, fb, :], parked[:, fb, :], FN.Gelu)
-            mlp_output(0, u_first)
+                u_first = hidden.tile([P, T], BF16, name="u_first", bufs=FB)
+                nc.scalar.activation(u_first[:], parked[:, fb, :], FN.Gelu)
+                for cb in range(CB):
+                    nc.tensor.matmul(
+                        sums[cb][:], fc2_sb[:, fb, cb * P : (cb + 1) * P], u_first[:],
+                        start=(fb == 0), stop=(fb == FB - 1),
+                    )
+            for cb in range(CB):
+                store(0, cb, sums[cb])
 
             u_second = hidden.tile([P, FB, T], BF16, name="u_second")
             for fb in range(FB):
-                u_ps = mlp_ps.tile([P, T], F32, name="u_ps", tag="mlp")
+                u_ps = qkv_ps.tile([P, T], F32, name="u_ps", tag="qkv")
                 hidden_sums(u_ps, 1, fb)
                 nc.scalar.activation(u_second[:, fb, :], u_ps[:], FN.Gelu)
             mlp_output(1, u_second)

@@ -227,10 +227,8 @@ def tile_tinygpt_ntp_b_kernel(
                 width = seen + P
                 q_blk = qk[s][:, 0, head, seen:width]
                 sc = att_ps.tile([P, T], F32, name="sc", bufs=3)
-                if jb > 0:
-                    nc.tensor.matmul(sc[:, 0:seen], q_blk, qk[s][:, 1, head, 0:seen], start=True, stop=True)
-                nc.tensor.matmul(sc[:, seen:width], ident[:], causal[:], start=True, stop=False)
-                nc.tensor.matmul(sc[:, seen:width], q_blk, qk[s][:, 1, head, seen:width], start=False, stop=True)
+                nc.tensor.matmul(sc[:, 0:width], q_blk, qk[s][:, 1, head, 0:width], start=True, stop=False)
+                nc.tensor.matmul(sc[:, seen:width], ident[:], causal[:], start=False, stop=True)
                 neg_max = soft.tile([P, 1], F32, name="neg_max")
                 nc.vector.reduce_max(neg_max[:], sc[:, 0:width], axis=AXIS_X, negate=True)
                 e = soft.tile([P, T], F32, name="e")

@@ -19,6 +19,7 @@ FB = F // P
 TB = T // P
 EPS = 1e-5
 HALF = T // 2
+WEIGHTS_LAG, FLIP_LAG = 1, 3
 MASKED = -1e30
 
 FLOPS = 2 * N * C * E + 4 * B * H * DH * (T * (T + 1) // 2) + 2 * N * C * C + 4 * N * C * F
@@ -86,14 +87,18 @@ def tile_tinygpt_ntp_b_kernel(
                 )
             return rstd
 
-        def layer_norm(x, n, s, first, width, v, banks, by_power=False):
+        def add_three(three, x, cols):
+            nc.vector.tensor_tensor(three[:], x[:, 0, cols], x[:, 1, cols], ALU.add)
+            nc.vector.tensor_tensor(three[:], three[:], x[:, 2, cols], ALU.add)
+
+        def layer_norm(x, n, s, first, width, v, banks, by_power=False, three=None):
             here = slice(first, first + width)
             cols = slice(s * T + first, s * T + first + width)
-            part = norm.tile([P, width], F32, name="part")
-            nc.vector.tensor_tensor(part[:], x[:, 0, cols], x[:, 1, cols], ALU.add)
-            nc.vector.tensor_tensor(part[:], part[:], x[:, 2, cols], ALU.add)
+            if three is None:
+                three = norm.tile([P, width], F32, name="three")
+                add_three(three, x, cols)
             total = norm.tile([P, width], BF16, name="total")
-            nc.vector.tensor_tensor(total[:], part[:], x[:, 3, cols], ALU.add)
+            nc.vector.tensor_tensor(total[:], three[:], x[:, 3, cols], ALU.add)
             mean = banks.tile([P, width], F32, name="mean", tag="stat")
             nc.tensor.matmul(mean[:], averager[:], total[:], start=True, stop=True)
             xc = norm.tile([P, CB, width], F32, name="xc")
@@ -114,7 +119,7 @@ def tile_tinygpt_ntp_b_kernel(
             for cb in range(CB):
                 gain = ln_cols[:, v * CB + cb : v * CB + cb + 1]
                 bias = ln_cols[:, (v + 1) * CB + cb : (v + 1) * CB + cb + 1]
-                xn = norm.tile([P, width], F32, name="xn", bufs=4)
+                xn = norm.tile([P, width], F32, name="xn", bufs=3)
                 nc.vector.tensor_tensor(xn[:], xc[:, cb, :], rstd[:, 0:width], ALU.mult)
                 if cb % 2 == 0:
                     nc.vector.tensor_scalar(n[:, cb, here], xn[:], gain, bias, op0=ALU.mult, op1=ALU.add)
@@ -144,6 +149,7 @@ def tile_tinygpt_ntp_b_kernel(
             ln_cols = held.tile([P, 4 * CB], F32, name="ln_cols")
             nc.vector.tensor_copy(ln_cols[:], ln_ps[:, 0 : 4 * CB])
 
+            three_next = norm.tile([P, T], F32, name="three_next", bufs=1)
             for first in range(0, N, HALF):
                 for cb in range(CB):
                     nc.vector.tensor_tensor(
@@ -153,7 +159,10 @@ def tile_tinygpt_ntp_b_kernel(
                         ALU.add,
                     )
                 if first < T:
-                    layer_norm(h0, n1[0], 0, first, HALF, 0, first_ps)
+                    three = norm.tile([P, HALF], F32, name="three")
+                    add_three(three, h0, slice(first, first + HALF))
+                    layer_norm(h0, n1[0], 0, first, HALF, 0, first_ps, three=three)
+            add_three(three_next, h0, slice(T, N))
 
         late = pools.enter_context(tc.tile_pool(name="late", bufs=1))
         h1 = late.tile([P, CB, N], F32, name="h1")
@@ -217,12 +226,12 @@ def tile_tinygpt_ntp_b_kernel(
             def park(fb):
                 u_ps = qkv_ps.tile([P, T], F32, name="u_ps", tag="qkv")
                 hidden_sums(u_ps, 0, fb)
-                if fb % 2 == 0:
+                if fb % 4 == 0:
                     nc.vector.tensor_copy(parked[:, fb, :], u_ps[:])
                 else:
                     nc.scalar.copy(parked[:, fb, :], u_ps[:])
 
-            def softmax_block(s, head, jb, p_t):
+            def scores(s, head, jb):
                 seen = jb * P
                 width = seen + P
                 q_blk = qk[s][:, 0, head, seen:width]
@@ -231,6 +240,9 @@ def tile_tinygpt_ntp_b_kernel(
                 nc.tensor.matmul(sc[:, seen:width], ident[:], causal[:], start=False, stop=True)
                 neg_max = soft.tile([P, 1], F32, name="neg_max")
                 nc.vector.reduce_max(neg_max[:], sc[:, 0:width], axis=AXIS_X, negate=True)
+                return sc, neg_max
+
+            def weights(sc, neg_max, width):
                 e = soft.tile([P, T], F32, name="e")
                 e_sum = soft.tile([P, 1], F32, name="e_sum")
                 nc.scalar.activation(
@@ -240,12 +252,15 @@ def tile_tinygpt_ntp_b_kernel(
                 nc.vector.reciprocal(inv_sum[:], e_sum[:])
                 p = soft.tile([P, T], BF16, name="p")
                 nc.vector.tensor_scalar_mul(p[:, 0:width], e[:, 0:width], inv_sum[:, 0:1])
+                return p
+
+            def flip(p, jb, p_t):
                 pt_ps = att_ps.tile([P, T], BF16, name="pt_ps")
                 for ib in range(jb + 1):
                     nc.tensor.transpose(pt_ps[:, ib * P : (ib + 1) * P], p[:, ib * P : (ib + 1) * P], ident[:])
                 nc.vector.tensor_copy(
-                    p_t[:, 0 : jb + 1, seen:width],
-                    pt_ps[:, 0:width].rearrange("i (ib j) -> i ib j", j=P),
+                    p_t[:, 0 : jb + 1, jb * P : (jb + 1) * P],
+                    pt_ps[:, 0 : (jb + 1) * P].rearrange("i (ib j) -> i ib j", j=P),
                 )
 
             def weighted_values(s, head, p_t):
@@ -258,22 +273,25 @@ def tile_tinygpt_ntp_b_kernel(
                 nc.scalar.copy(o[s][:, head, :], o_ps[:])
 
             def attention(s, groups):
-                ready = None
-                for head in range(H):
-                    p_t = soft.tile([P, TB, T], BF16, name="p_t", bufs=2)
-                    for jb in range(TB):
-                        softmax_block(s, head, jb, p_t)
-                        block = head * TB + jb
-                        if block < len(groups):
-                            for piece in groups[block]:
-                                piece()
-                        if ready is not None and jb == TB - 1:
-                            weighted_values(s, *ready)
-                    ready = (head, p_t)
-                for group in groups[H * TB :]:
-                    for piece in group:
-                        piece()
-                weighted_values(s, *ready)
+                blocks = H * TB
+                scored, weighed, flipped = {}, {}, {}
+                for step in range(max(blocks + FLIP_LAG, len(groups))):
+                    if step < blocks:
+                        scored[step] = scores(s, step // TB, step % TB)
+                    block = step - WEIGHTS_LAG
+                    if 0 <= block < blocks:
+                        weighed[block] = weights(*scored[block], (block % TB + 1) * P)
+                    block = step - FLIP_LAG
+                    if 0 <= block < blocks:
+                        head, jb = block // TB, block % TB
+                        if jb == 0:
+                            flipped[head] = soft.tile([P, TB, T], BF16, name="p_t", bufs=2)
+                        flip(weighed[block], jb, flipped[head])
+                    if step < len(groups):
+                        for piece in groups[step]:
+                            piece()
+                    if 0 <= block < blocks and block % TB == TB - 1:
+                        weighted_values(s, block // TB, flipped[block // TB])
 
             for first in (0, HALF):
                 project_qk(0, 0, first)
@@ -282,23 +300,22 @@ def tile_tinygpt_ntp_b_kernel(
             own = [partial(project_whole, 0, 1, which) for which in (0, 1)]
             own += [partial(project_v, 0, tb) for tb in range(TB)]
             own += [partial(project_whole, 0, head, which) for head in (2, 3) for which in (0, 1)]
-            groups = [[piece] for piece in own]
-            groups[2] += [partial(layer_norm, h0, n1[1], 1, 0, T, 0, stat_ps, by_power=True)]
+            following = [partial(project_whole, 1, head, which) for head in (0, 1) for which in (0, 1)]
+            following += [partial(project_v, 1, tb) for tb in range(TB)]
+            following += [partial(project_whole, 1, head, which) for head in (2, 3) for which in (0, 1)]
+            groups = [[piece] for piece in own] + [[] for block in range(H * TB - len(own))]
+            groups[0] += [partial(layer_norm, h0, n1[1], 1, 0, T, 0, stat_ps, by_power=True, three=three_next)]
+            for tb in range(TB):
+                groups[(H - 1) * TB + tb] += [following[tb]]
             attention(0, groups)
-
             for cb in range(CB):
                 project_out(0, cb)
-                if cb % 2 == 0:
-                    for which in range(2):
-                        project_whole(1, cb // 2, which)
-                else:
-                    for tb in (cb - 1, cb):
-                        project_v(1, tb)
             layer_norm(h1, n2[0], 0, 0, T, 2, stat_ps, by_power=True)
 
-            rest = [partial(project_whole, 1, head, which) for head in (2, 3) for which in (0, 1)]
-            rest += [partial(park, fb) for fb in range(FB)]
-            attention(1, [[piece] for piece in rest])
+            for piece in following[TB : TB + 2]:
+                piece()
+            pieces = following[TB + 2 :] + [partial(park, fb) for fb in range(FB)]
+            attention(1, [[piece] for piece in pieces])
             for cb in range(CB):
                 project_out(1, cb)
             layer_norm(h1, n2[1], 1, 0, T, 2, stat_ps)

@@ -19,6 +19,7 @@ FB = F // P
 TB = T // P
 EPS = 1e-5
 HALF = T // 2
+PARKED = H * TB - 4
 WEIGHTS_LAG, FLIP_LAG = 1, 3
 MASKED = -1e30
 
@@ -87,20 +88,21 @@ def tile_tinygpt_ntp_b_kernel(
                 )
             return rstd
 
-        def add_three(three, x, cols):
-            nc.vector.tensor_tensor(three[:], x[:, 0, cols], x[:, 1, cols], ALU.add)
-            nc.vector.tensor_tensor(three[:], three[:], x[:, 2, cols], ALU.add)
+        def channel_mean(x, s, banks, three=None):
+            cols = slice(s * T, (s + 1) * T)
+            if three is None:
+                three = norm.tile([P, T], F32, name="three")
+                nc.vector.tensor_tensor(three[:], x[:, 0, cols], x[:, 1, cols], ALU.add)
+                nc.vector.tensor_tensor(three[:], three[:], x[:, 2, cols], ALU.add)
+            total = norm.tile([P, T], BF16, name="total")
+            nc.vector.tensor_tensor(total[:], three[:], x[:, 3, cols], ALU.add)
+            mean = banks.tile([P, T], F32, name="mean", tag="stat")
+            nc.tensor.matmul(mean[:], averager[:], total[:], start=True, stop=True)
+            return mean
 
-        def layer_norm(x, n, s, first, width, v, banks, by_power=False, three=None):
+        def layer_norm(x, mean, n, s, first, width, v, banks, by_power=False):
             here = slice(first, first + width)
             cols = slice(s * T + first, s * T + first + width)
-            if three is None:
-                three = norm.tile([P, width], F32, name="three")
-                add_three(three, x, cols)
-            total = norm.tile([P, width], BF16, name="total")
-            nc.vector.tensor_tensor(total[:], three[:], x[:, 3, cols], ALU.add)
-            mean = banks.tile([P, width], F32, name="mean", tag="stat")
-            nc.tensor.matmul(mean[:], averager[:], total[:], start=True, stop=True)
             xc = norm.tile([P, CB, width], F32, name="xc")
             squares = []
             for cb in range(CB):
@@ -149,20 +151,29 @@ def tile_tinygpt_ntp_b_kernel(
             ln_cols = held.tile([P, 4 * CB], F32, name="ln_cols")
             nc.vector.tensor_copy(ln_cols[:], ln_ps[:, 0 : 4 * CB])
 
-            three_next = norm.tile([P, T], F32, name="three_next", bufs=1)
+            three = norm.tile([P, T], F32, name="three")
             for first in range(0, N, HALF):
+                cols = slice(first, first + HALF)
                 for cb in range(CB):
                     nc.vector.tensor_tensor(
-                        h0[:, cb, first : first + HALF],
+                        h0[:, cb, cols],
                         tok[cb][:].indirect(offsets[:, first // 16 : (first + HALF) // 16]),
                         pos_sb[:, cb, first % T : first % T + HALF],
                         ALU.add,
                     )
                 if first < T:
-                    three = norm.tile([P, HALF], F32, name="three")
-                    add_three(three, h0, slice(first, first + HALF))
-                    layer_norm(h0, n1[0], 0, first, HALF, 0, first_ps, three=three)
-            add_three(three_next, h0, slice(T, N))
+                    two = norm.tile([P, HALF], F32, name="two")
+                    nc.vector.tensor_tensor(two[:], h0[:, 0, cols], h0[:, 1, cols], ALU.add)
+                    rounded = norm.tile([P, HALF], BF16, name="rounded")
+                    nc.vector.tensor_tensor(rounded[:], two[:], h0[:, 2, cols], ALU.add)
+                    last = norm.tile([P, HALF], BF16, name="last")
+                    nc.scalar.copy(last[:], h0[:, 3, cols])
+                    mean = first_ps.tile([P, HALF], F32, name="mean", tag="stat")
+                    nc.tensor.matmul(mean[:], averager[:], rounded[:], start=True, stop=False)
+                    nc.tensor.matmul(mean[:], averager[:], last[:], start=False, stop=True)
+                    layer_norm(h0, mean, n1[0], 0, first, HALF, 0, first_ps)
+            nc.vector.tensor_tensor(three[:], h0[:, 0, T:N], h0[:, 1, T:N], ALU.add)
+            nc.vector.tensor_tensor(three[:], three[:], h0[:, 2, T:N], ALU.add)
 
         late = pools.enter_context(tc.tile_pool(name="late", bufs=1))
         h1 = late.tile([P, CB, N], F32, name="h1")
@@ -170,7 +181,7 @@ def tile_tinygpt_ntp_b_kernel(
         v_t = [late.tile([P, TB, C], BF16, name=f"v_t{s}") for s in range(B)]
         o = [late.tile([P, H, T], BF16, name=f"o{s}") for s in range(B)]
         n2 = [late.tile([P, CB, T], BF16, name=f"n2_{s}") for s in range(B)]
-        parked = late.tile([P, FB, T], F32, name="parked")
+        parked = late.tile([P, PARKED, T], F32, name="parked")
 
         def project_out(s, cb):
             cols = slice(s * T, (s + 1) * T)
@@ -293,55 +304,64 @@ def tile_tinygpt_ntp_b_kernel(
                     if 0 <= block < blocks and block % TB == TB - 1:
                         weighted_values(s, block // TB, flipped[block // TB])
 
-            for first in (0, HALF):
-                project_qk(0, 0, first)
-            warm_exp = soft.tile([P, 1], F32, name="warm_exp", bufs=1)
-            nc.scalar.activation(warm_exp[:], qk[0][:, 0, 0, 0:1], FN.Exp)
+            project_qk(0, 0, 0)
+            project_v(0, 0)
+            project_qk(0, 0, HALF)
+            def first_norm():
+                layer_norm(h0, channel_mean(h0, 1, stat_ps, three), n1[1], 1, 0, T, 0, stat_ps, by_power=True)
+
             own = [partial(project_whole, 0, 1, which) for which in (0, 1)]
-            own += [partial(project_v, 0, tb) for tb in range(TB)]
+            own += [partial(project_v, 0, tb) for tb in (1, 2, 3)]
             own += [partial(project_whole, 0, head, which) for head in (2, 3) for which in (0, 1)]
             following = [partial(project_whole, 1, head, which) for head in (0, 1) for which in (0, 1)]
             following += [partial(project_v, 1, tb) for tb in range(TB)]
             following += [partial(project_whole, 1, head, which) for head in (2, 3) for which in (0, 1)]
             groups = [[piece] for piece in own] + [[] for block in range(H * TB - len(own))]
-            groups[0] += [partial(layer_norm, h0, n1[1], 1, 0, T, 0, stat_ps, by_power=True, three=three_next)]
+            groups[0] += [first_norm]
             for tb in range(TB):
                 groups[(H - 1) * TB + tb] += [following[tb]]
             attention(0, groups)
             for cb in range(CB):
                 project_out(0, cb)
-            layer_norm(h1, n2[0], 0, 0, T, 2, stat_ps, by_power=True)
+            layer_norm(h1, channel_mean(h1, 0, stat_ps), n2[0], 0, 0, T, 2, stat_ps, by_power=True)
 
             for piece in following[TB : TB + 2]:
                 piece()
-            pieces = following[TB + 2 :] + [partial(park, fb) for fb in range(FB)]
+            pieces = following[TB + 2 :] + [partial(park, fb) for fb in range(PARKED)]
             attention(1, [[piece] for piece in pieces])
             for cb in range(CB):
                 project_out(1, cb)
-            layer_norm(h1, n2[1], 1, 0, T, 2, stat_ps)
+            layer_norm(h1, channel_mean(h1, 1, stat_ps), n2[1], 1, 0, T, 2, stat_ps)
 
         with tc.tile_pool(name="hidden", bufs=1) as hidden, tc.psum_pool(name="mlp_ps", bufs=4) as mlp_ps:
 
-            def store(s, cb, y_ps):
-                cols = slice(s * T, (s + 1) * T)
-                y = late.tile([P, T], F32, name="y", bufs=3)
+            def store(s, cb, y_ps, first=0, width=T):
+                cols = slice(s * T + first, s * T + first + width)
+                y = late.tile([P, width], F32, name="y", bufs=3)
                 nc.vector.tensor_tensor(y[:], h1[:, cb, cols], y_ps[:], ALU.add)
                 nc.sync.dma_start(out[cb * P : (cb + 1) * P, cols], y[:])
 
             def mlp_output(s, u):
                 for cb in range(CB):
-                    y_ps = mlp_ps.tile([P, T], F32, name="y_ps", tag="mlp")
-                    for fb in range(FB):
-                        nc.tensor.matmul(
-                            y_ps[:], fc2_sb[:, fb, cb * P : (cb + 1) * P], u[:, fb, :],
-                            start=(fb == 0), stop=(fb == FB - 1),
-                        )
-                    store(s, cb, y_ps)
+                    width = HALF if cb == CB - 1 else T
+                    for first in range(0, T, width):
+                        y_ps = mlp_ps.tile([P, width], F32, name="y_ps", tag="mlp")
+                        for fb in range(FB):
+                            nc.tensor.matmul(
+                                y_ps[:], fc2_sb[:, fb, cb * P : (cb + 1) * P], u[:, fb, first : first + width],
+                                start=(fb == 0), stop=(fb == FB - 1),
+                            )
+                        store(s, cb, y_ps, first, width)
 
             sums = [mlp_ps.tile([P, T], F32, name=f"y_ps{cb}", tag="mlp") for cb in range(CB)]
             for fb in range(FB):
                 u_first = hidden.tile([P, T], BF16, name="u_first", bufs=FB)
-                nc.scalar.activation(u_first[:], parked[:, fb, :], FN.Gelu)
+                if fb < PARKED:
+                    nc.scalar.activation(u_first[:], parked[:, fb, :], FN.Gelu)
+                else:
+                    u_ps = qkv_ps.tile([P, T], F32, name="u_ps", tag="qkv")
+                    hidden_sums(u_ps, 0, fb)
+                    nc.scalar.activation(u_first[:], u_ps[:], FN.Gelu)
                 for cb in range(CB):
                     nc.tensor.matmul(
                         sums[cb][:], fc2_sb[:, fb, cb * P : (cb + 1) * P], u_first[:],

@@ -19,7 +19,7 @@ FB = F // P
 TB = T // P
 EPS = 1e-5
 HALF = T // 2
-PARKED = H * TB - 4
+PARKED = 12
 WEIGHTS_LAG, FLIP_LAG = 1, 3
 MASKED = -1e30
 
@@ -81,11 +81,14 @@ def tile_tinygpt_ntp_b_kernel(
             column = norm.tile([P, TB], F32, name="column")
             nc.gpsimd.tensor_tensor(column[:, 0:blocks], var_eps[:, 0:blocks], minus_half[:, 0:blocks], ALU.pow)
             rstd = banks.tile([P, T], F32, name="rstd_rows", tag="stat")
+            high = norm.tile([P, TB], BF16, name="high")
+            nc.vector.tensor_copy(high[:, 0:blocks], column[:, 0:blocks])
+            low = norm.tile([P, TB], BF16, name="low")
+            nc.vector.tensor_tensor(low[:, 0:blocks], column[:, 0:blocks], high[:, 0:blocks], ALU.subtract)
             for jb in range(blocks):
-                nc.tensor.matmul(
-                    rstd[:, jb * P : (jb + 1) * P], column[:, jb : jb + 1].to_broadcast([P, P]), ident_f32[:],
-                    start=True, stop=True,
-                )
+                row = rstd[:, jb * P : (jb + 1) * P]
+                nc.tensor.matmul(row, high[:, jb : jb + 1].to_broadcast([P, P]), ident[:], start=True, stop=False)
+                nc.tensor.matmul(row, low[:, jb : jb + 1].to_broadcast([P, P]), ident[:], start=False, stop=True)
             return rstd
 
         def channel_mean(x, s, banks, three=None):
@@ -151,27 +154,31 @@ def tile_tinygpt_ntp_b_kernel(
             ln_cols = held.tile([P, 4 * CB], F32, name="ln_cols")
             nc.vector.tensor_copy(ln_cols[:], ln_ps[:, 0 : 4 * CB])
 
-            three = norm.tile([P, T], F32, name="three")
-            for first in range(0, N, HALF):
-                cols = slice(first, first + HALF)
+            def look_up(first, width):
                 for cb in range(CB):
                     nc.vector.tensor_tensor(
-                        h0[:, cb, cols],
-                        tok[cb][:].indirect(offsets[:, first // 16 : (first + HALF) // 16]),
-                        pos_sb[:, cb, first % T : first % T + HALF],
+                        h0[:, cb, first : first + width],
+                        tok[cb][:].indirect(offsets[:, first // 16 : (first + width) // 16]),
+                        pos_sb[:, cb, first % T : first % T + width],
                         ALU.add,
                     )
-                if first < T:
-                    two = norm.tile([P, HALF], F32, name="two")
-                    nc.vector.tensor_tensor(two[:], h0[:, 0, cols], h0[:, 1, cols], ALU.add)
-                    rounded = norm.tile([P, HALF], BF16, name="rounded")
-                    nc.vector.tensor_tensor(rounded[:], two[:], h0[:, 2, cols], ALU.add)
-                    last = norm.tile([P, HALF], BF16, name="last")
-                    nc.scalar.copy(last[:], h0[:, 3, cols])
-                    mean = first_ps.tile([P, HALF], F32, name="mean", tag="stat")
-                    nc.tensor.matmul(mean[:], averager[:], rounded[:], start=True, stop=False)
-                    nc.tensor.matmul(mean[:], averager[:], last[:], start=False, stop=True)
-                    layer_norm(h0, mean, n1[0], 0, first, HALF, 0, first_ps)
+
+            for first in (0, HALF):
+                cols = slice(first, first + HALF)
+                look_up(first, HALF)
+                two = norm.tile([P, HALF], F32, name="two")
+                nc.vector.tensor_tensor(two[:], h0[:, 0, cols], h0[:, 1, cols], ALU.add)
+                rounded = norm.tile([P, HALF], BF16, name="rounded")
+                nc.vector.tensor_tensor(rounded[:], two[:], h0[:, 2, cols], ALU.add)
+                last = norm.tile([P, HALF], BF16, name="last")
+                nc.scalar.copy(last[:], h0[:, 3, cols])
+                mean = first_ps.tile([P, HALF], F32, name="mean", tag="stat")
+                nc.tensor.matmul(mean[:], averager[:], rounded[:], start=True, stop=False)
+                nc.tensor.matmul(mean[:], averager[:], last[:], start=False, stop=True)
+                layer_norm(h0, mean, n1[0], 0, first, HALF, 0, first_ps)
+            for first in range(T, N, P):
+                look_up(first, P)
+            three = norm.tile([P, T], F32, name="three")
             nc.vector.tensor_tensor(three[:], h0[:, 0, T:N], h0[:, 1, T:N], ALU.add)
             nc.vector.tensor_tensor(three[:], three[:], h0[:, 2, T:N], ALU.add)
 
@@ -237,10 +244,7 @@ def tile_tinygpt_ntp_b_kernel(
             def park(fb):
                 u_ps = qkv_ps.tile([P, T], F32, name="u_ps", tag="qkv")
                 hidden_sums(u_ps, 0, fb)
-                if fb % 4 == 0:
-                    nc.vector.tensor_copy(parked[:, fb, :], u_ps[:])
-                else:
-                    nc.scalar.copy(parked[:, fb, :], u_ps[:])
+                nc.scalar.copy(parked[:, fb, :], u_ps[:])
 
             def scores(s, head, jb):
                 seen = jb * P
@@ -325,9 +329,7 @@ def tile_tinygpt_ntp_b_kernel(
                 project_out(0, cb)
             layer_norm(h1, channel_mean(h1, 0, stat_ps), n2[0], 0, 0, T, 2, stat_ps, by_power=True)
 
-            for piece in following[TB : TB + 2]:
-                piece()
-            pieces = following[TB + 2 :] + [partial(park, fb) for fb in range(PARKED)]
+            pieces = following[TB:] + [partial(park, fb) for fb in range(PARKED)]
             attention(1, [[piece] for piece in pieces])
             for cb in range(CB):
                 project_out(1, cb)

@@ -20,7 +20,7 @@ TB = T // P
 EPS = 1e-5
 HALF = T // 2
 PARKED = 12
-WEIGHTS_LAG, FLIP_LAG = 1, 3
+WEIGHTS_LAG, FLIP_LAG = 2, 3
 MASKED = -1e30
 
 FLOPS = 2 * N * C * E + 4 * B * H * DH * (T * (T + 1) // 2) + 2 * N * C * C + 4 * N * C * F
@@ -345,8 +345,8 @@ def tile_tinygpt_ntp_b_kernel(
 
             def mlp_output(s, u):
                 for cb in range(CB):
-                    width = HALF if cb == CB - 1 else T
-                    for first in range(0, T, width):
+                    parts = ((0, T - P), (T - P, P)) if cb == CB - 1 else ((0, T),)
+                    for first, width in parts:
                         y_ps = mlp_ps.tile([P, width], F32, name="y_ps", tag="mlp")
                         for fb in range(FB):
                             nc.tensor.matmul(

@@ -289,17 +289,18 @@ def tile_tinygpt_ntp_b_kernel(
 
             def attention(s, groups):
                 blocks = H * TB
+                order = [(head, jb) for head in range(H) for jb in (range(TB - 1, -1, -1) if head == H - 1 else range(TB))]
                 scored, weighed, flipped = {}, {}, {}
                 for step in range(max(blocks + FLIP_LAG, len(groups))):
                     if step < blocks:
-                        scored[step] = scores(s, step // TB, step % TB)
+                        scored[step] = scores(s, *order[step])
                     block = step - WEIGHTS_LAG
                     if 0 <= block < blocks:
-                        weighed[block] = weights(*scored[block], (block % TB + 1) * P)
+                        weighed[block] = weights(*scored[block], (order[block][1] + 1) * P)
                     block = step - FLIP_LAG
                     if 0 <= block < blocks:
-                        head, jb = block // TB, block % TB
-                        if jb == 0:
+                        head, jb = order[block]
+                        if block % TB == 0:
                             flipped[head] = soft.tile([P, TB, T], BF16, name="p_t", bufs=2)
                         flip(weighed[block], jb, flipped[head])
                     if step < len(groups):

from contextlib import ExitStack
from functools import partial

import concourse.mybir as mybir
from concourse.masks import make_identity

F32 = mybir.dt.float32
BF16 = mybir.dt.bfloat16
U16 = mybir.dt.uint16
I32 = mybir.dt.int32
ALU = mybir.AluOpType
FN = mybir.ActivationFunctionType
AXIS_X = mybir.AxisListType.X

P = 128
C, S, N, B, T, H, DH, E, F = 512, 4096, 1024, 2, 512, 4, 128, 1536, 2048
CB = C // P
FB = F // P
TB = T // P
EPS = 1e-5
HALF = T // 2
PARKED = 12
WEIGHTS_LAG, FLIP_LAG = 2, 3
MASKED = -1e30

FLOPS = 2 * N * C * E + 4 * B * H * DH * (T * (T + 1) // 2) + 2 * N * C * C + 4 * N * C * F


def tile_tinygpt_ntp_b_kernel(
    tc, tok_emb, pos_emb, ln1_w, ln1_b, qkv_w, proj_w, ln2_w, ln2_b, fc1_w, fc2_w, offs, out
):
    nc = tc.nc
    with ExitStack() as pools:
        held = pools.enter_context(tc.tile_pool(name="held", bufs=1))
        norm = pools.enter_context(tc.tile_pool(name="norm", bufs=2))
        stat_ps = pools.enter_context(tc.psum_pool(name="stat_ps", bufs=2))
        qkv_ps = pools.enter_context(tc.psum_pool(name="qkv_ps", bufs=2))

        offsets = held.tile([P, N // 16], U16, name="offsets")
        nc.sync.dma_start(offsets[:], offs)

        ident = held.tile([P, P], BF16, name="ident")
        make_identity(nc, ident[:])
        ident64 = held.tile([64, 64], F32, name="ident64")
        make_identity(nc, ident64[:])
        ahead = held.tile([P, P], I32, name="ahead")
        nc.gpsimd.iota(ahead[:], pattern=[[1, P]], base=0, channel_multiplier=-1)
        causal = held.tile([P, P], BF16, name="causal")
        nc.vector.tensor_scalar(causal[:], ahead[:], 0.0, MASKED, op0=ALU.is_gt, op1=ALU.mult)
        averager = held.tile([P, P], BF16, name="averager")
        nc.vector.memset(averager[:], 1.0 / C)
        mean_column = held.tile([P, 1], BF16, name="mean_column")
        nc.vector.memset(mean_column[:], 1.0 / C)
        ident_f32 = held.tile([P, P], F32, name="ident_f32")
        make_identity(nc, ident_f32[:])
        minus_half = held.tile([P, TB], F32, name="minus_half")
        nc.vector.memset(minus_half[:], -0.5)
        eps = held.tile([P, 1], F32, name="eps")
        nc.vector.memset(eps[:], EPS)
        warm = held.tile([P, 1], F32, name="warm")
        nc.scalar.activation(warm[:], eps[:], FN.Abs_reciprocal_sqrt)

        h0 = held.tile([P, CB, N], F32, name="h0")
        ln_rows = held.tile([64, P], F32, name="ln_rows")
        qkv_sb = held.tile([P, CB, E], BF16, name="qkv_sb")
        proj_sb = held.tile([P, CB, C], BF16, name="proj_sb")
        fc1_sb = held.tile([P, CB, F], BF16, name="fc1_sb")
        fc2_sb = held.tile([P, FB, C], BF16, name="fc2_sb")

        def rstd_by_power(squares, width, banks):
            blocks = width // P
            var = banks.tile([P, TB], F32, name="var_columns", tag="stat")
            for jb in range(blocks):
                for cb in range(CB):
                    nc.tensor.matmul(
                        var[:, jb : jb + 1], squares[cb][:, jb * P : (jb + 1) * P], mean_column[:],
                        start=(cb == 0), stop=(cb == CB - 1),
                    )
            var_eps = norm.tile([P, TB], F32, name="var_eps")
            nc.vector.tensor_scalar_add(var_eps[:, 0:blocks], var[:, 0:blocks], EPS)
            column = norm.tile([P, TB], F32, name="column")
            nc.gpsimd.tensor_tensor(column[:, 0:blocks], var_eps[:, 0:blocks], minus_half[:, 0:blocks], ALU.pow)
            rstd = banks.tile([P, T], F32, name="rstd_rows", tag="stat")
            high = norm.tile([P, TB], BF16, name="high")
            nc.vector.tensor_copy(high[:, 0:blocks], column[:, 0:blocks])
            low = norm.tile([P, TB], BF16, name="low")
            nc.vector.tensor_tensor(low[:, 0:blocks], column[:, 0:blocks], high[:, 0:blocks], ALU.subtract)
            for jb in range(blocks):
                row = rstd[:, jb * P : (jb + 1) * P]
                nc.tensor.matmul(row, high[:, jb : jb + 1].to_broadcast([P, P]), ident[:], start=True, stop=False)
                nc.tensor.matmul(row, low[:, jb : jb + 1].to_broadcast([P, P]), ident[:], start=False, stop=True)
            return rstd

        def channel_mean(x, s, banks, three=None):
            cols = slice(s * T, (s + 1) * T)
            if three is None:
                three = norm.tile([P, T], F32, name="three")
                nc.vector.tensor_tensor(three[:], x[:, 0, cols], x[:, 1, cols], ALU.add)
                nc.vector.tensor_tensor(three[:], three[:], x[:, 2, cols], ALU.add)
            total = norm.tile([P, T], BF16, name="total")
            nc.vector.tensor_tensor(total[:], three[:], x[:, 3, cols], ALU.add)
            mean = banks.tile([P, T], F32, name="mean", tag="stat")
            nc.tensor.matmul(mean[:], averager[:], total[:], start=True, stop=True)
            return mean

        def layer_norm(x, mean, n, s, first, width, v, banks, by_power=False):
            here = slice(first, first + width)
            cols = slice(s * T + first, s * T + first + width)
            xc = norm.tile([P, CB, width], F32, name="xc")
            squares = []
            for cb in range(CB):
                nc.vector.tensor_tensor(xc[:, cb, :], x[:, cb, cols], mean[:], ALU.subtract)
                sq = norm.tile([P, width], BF16, name="sq", bufs=CB)
                nc.scalar.square(sq[:], xc[:, cb, :])
                squares.append(sq)
            if by_power:
                rstd = rstd_by_power(squares, width, banks)
            else:
                var = banks.tile([P, width], F32, name="var", tag="stat")
                for cb in range(CB):
                    nc.tensor.matmul(var[:], averager[:], squares[cb][:], start=(cb == 0), stop=(cb == CB - 1))
                rstd = norm.tile([P, width], F32, name="rstd")
                nc.scalar.activation(rstd[:], var[:], FN.Abs_reciprocal_sqrt, bias=eps[:, 0:1])
            for cb in range(CB):
                gain = ln_cols[:, v * CB + cb : v * CB + cb + 1]
                bias = ln_cols[:, (v + 1) * CB + cb : (v + 1) * CB + cb + 1]
                xn = norm.tile([P, width], F32, name="xn", bufs=3)
                nc.vector.tensor_tensor(xn[:], xc[:, cb, :], rstd[:, 0:width], ALU.mult)
                if cb % 2 == 0:
                    nc.vector.tensor_scalar(n[:, cb, here], xn[:], gain, bias, op0=ALU.mult, op1=ALU.add)
                else:
                    nc.scalar.activation(n[:, cb, here], xn[:], FN.Identity, bias=bias, scale=gain)

        n1 = [held.tile([P, CB, T], BF16, name=f"n1_{s}") for s in range(B)]
        with tc.tile_pool(name="table", bufs=1) as table, tc.psum_pool(name="first_ps", bufs=4) as first_ps:
            pos_sb = table.tile([P, CB, T], F32, name="pos_sb")
            nc.scalar.dma_start(pos_sb[:], pos_emb.rearrange("(cb p) t -> p cb t", p=P))
            tok = []
            for cb in range(CB):
                tok_cb = table.tile([P, S], F32, name=f"tok{cb}")
                nc.sync.dma_start(tok_cb[:], tok_emb[cb * P : (cb + 1) * P, :])
                tok.append(tok_cb)
            nc.sync.dma_start(qkv_sb[:], qkv_w.rearrange("(cb p) e -> p cb e", p=P))
            nc.sync.dma_start(proj_sb[:], proj_w.rearrange("(cb p) c -> p cb c", p=P))
            nc.sync.dma_start(fc1_sb[:], fc1_w.rearrange("(cb p) f -> p cb f", p=P))
            nc.sync.dma_start(fc2_sb[:], fc2_w.rearrange("(fb p) c -> p fb c", p=P))
            nc.vector.memset(ln_rows[:], 0.0)
            for v, vec in enumerate((ln1_w, ln1_b, ln2_w, ln2_b)):
                nc.scalar.dma_start(
                    ln_rows[v * CB : (v + 1) * CB, :], vec.rearrange("(cb p) o -> cb (p o)", p=P)
                )
            ln_ps = stat_ps.tile([P, T], F32, name="ln_ps", tag="stat")
            nc.tensor.transpose(ln_ps[:, 0:64], ln_rows[:], ident64[:])
            ln_cols = held.tile([P, 4 * CB], F32, name="ln_cols")
            nc.vector.tensor_copy(ln_cols[:], ln_ps[:, 0 : 4 * CB])

            def look_up(first, width):
                for cb in range(CB):
                    nc.vector.tensor_tensor(
                        h0[:, cb, first : first + width],
                        tok[cb][:].indirect(offsets[:, first // 16 : (first + width) // 16]),
                        pos_sb[:, cb, first % T : first % T + width],
                        ALU.add,
                    )

            for first in (0, HALF):
                cols = slice(first, first + HALF)
                look_up(first, HALF)
                two = norm.tile([P, HALF], F32, name="two")
                nc.vector.tensor_tensor(two[:], h0[:, 0, cols], h0[:, 1, cols], ALU.add)
                rounded = norm.tile([P, HALF], BF16, name="rounded")
                nc.vector.tensor_tensor(rounded[:], two[:], h0[:, 2, cols], ALU.add)
                last = norm.tile([P, HALF], BF16, name="last")
                nc.scalar.copy(last[:], h0[:, 3, cols])
                mean = first_ps.tile([P, HALF], F32, name="mean", tag="stat")
                nc.tensor.matmul(mean[:], averager[:], rounded[:], start=True, stop=False)
                nc.tensor.matmul(mean[:], averager[:], last[:], start=False, stop=True)
                layer_norm(h0, mean, n1[0], 0, first, HALF, 0, first_ps)
            for first in range(T, N, P):
                look_up(first, P)
            three = norm.tile([P, T], F32, name="three")
            nc.vector.tensor_tensor(three[:], h0[:, 0, T:N], h0[:, 1, T:N], ALU.add)
            nc.vector.tensor_tensor(three[:], three[:], h0[:, 2, T:N], ALU.add)

        late = pools.enter_context(tc.tile_pool(name="late", bufs=1))
        h1 = late.tile([P, CB, N], F32, name="h1")
        qk = [late.tile([P, 2, H, T], BF16, name=f"qk{s}") for s in range(B)]
        v_t = [late.tile([P, TB, C], BF16, name=f"v_t{s}") for s in range(B)]
        o = [late.tile([P, H, T], BF16, name=f"o{s}") for s in range(B)]
        n2 = [late.tile([P, CB, T], BF16, name=f"n2_{s}") for s in range(B)]
        parked = late.tile([P, PARKED, T], F32, name="parked")

        def project_out(s, cb):
            cols = slice(s * T, (s + 1) * T)
            h_ps = stat_ps.tile([P, T], F32, name="h_ps", tag="stat")
            for head in range(H):
                nc.tensor.matmul(
                    h_ps[:], proj_sb[:, head, cb * P : (cb + 1) * P], o[s][:, head, :],
                    start=(head == 0), stop=(head == H - 1),
                )
            nc.vector.tensor_tensor(h1[:, cb, cols], h0[:, cb, cols], h_ps[:], ALU.add)

        def hidden_sums(u_ps, s, fb):
            for cb in range(CB):
                nc.tensor.matmul(
                    u_ps[:], fc1_sb[:, cb, fb * P : (fb + 1) * P], n2[s][:, cb, :],
                    start=(cb == 0), stop=(cb == CB - 1),
                )

        with ExitStack() as attention_pools:
            soft = attention_pools.enter_context(tc.tile_pool(name="soft", bufs=4))
            att_ps = attention_pools.enter_context(tc.psum_pool(name="att_ps", bufs=1))

            def project_qk(s, head, first):
                half = slice(first, first + HALF)
                qk_ps = qkv_ps.tile([P, 2, HALF], F32, name="qk_ps", tag="qkv")
                for which in range(2):
                    row0 = which * C + head * DH
                    for cb in range(CB):
                        nc.tensor.matmul(
                            qk_ps[:, which, :], qkv_sb[:, cb, row0 : row0 + DH], n1[s][:, cb, half],
                            start=(cb == 0), stop=(cb == CB - 1),
                        )
                nc.scalar.mul(qk[s][:, :, head, half], qk_ps[:], DH ** -0.25)

            def project_whole(s, head, which):
                row0 = which * C + head * DH
                qk_ps = qkv_ps.tile([P, T], F32, name="qk_ps", tag="qkv")
                for cb in range(CB):
                    nc.tensor.matmul(
                        qk_ps[:], qkv_sb[:, cb, row0 : row0 + DH], n1[s][:, cb, :], start=(cb == 0), stop=(cb == CB - 1),
                    )
                nc.scalar.mul(qk[s][:, which, head, :], qk_ps[:], DH ** -0.25)

            def project_v(s, tb):
                v_ps = qkv_ps.tile([P, C], F32, name="v_ps", tag="qkv")
                for cb in range(CB):
                    nc.tensor.matmul(
                        v_ps[:], n1[s][:, cb, tb * P : (tb + 1) * P], qkv_sb[:, cb, 2 * C : 3 * C],
                        start=(cb == 0), stop=(cb == CB - 1),
                    )
                nc.scalar.copy(v_t[s][:, tb, :], v_ps[:])

            def park(fb):
                u_ps = qkv_ps.tile([P, T], F32, name="u_ps", tag="qkv")
                hidden_sums(u_ps, 0, fb)
                nc.scalar.copy(parked[:, fb, :], u_ps[:])

            def scores(s, head, jb):
                seen = jb * P
                width = seen + P
                q_blk = qk[s][:, 0, head, seen:width]
                sc = att_ps.tile([P, T], F32, name="sc", bufs=3)
                nc.tensor.matmul(sc[:, 0:width], q_blk, qk[s][:, 1, head, 0:width], start=True, stop=False)
                nc.tensor.matmul(sc[:, seen:width], ident[:], causal[:], start=False, stop=True)
                neg_max = soft.tile([P, 1], F32, name="neg_max")
                nc.vector.reduce_max(neg_max[:], sc[:, 0:width], axis=AXIS_X, negate=True)
                return sc, neg_max

            def weights(sc, neg_max, width):
                e = soft.tile([P, T], F32, name="e")
                e_sum = soft.tile([P, 1], F32, name="e_sum")
                nc.scalar.activation(
                    e[:, 0:width], sc[:, 0:width], FN.Exp, bias=neg_max[:, 0:1], accum_out=e_sum[:, 0:1]
                )
                inv_sum = soft.tile([P, 1], F32, name="inv_sum")
                nc.vector.reciprocal(inv_sum[:], e_sum[:])
                p = soft.tile([P, T], BF16, name="p")
                nc.vector.tensor_scalar_mul(p[:, 0:width], e[:, 0:width], inv_sum[:, 0:1])
                return p

            def flip(p, jb, p_t):
                pt_ps = att_ps.tile([P, T], BF16, name="pt_ps")
                for ib in range(jb + 1):
                    nc.tensor.transpose(pt_ps[:, ib * P : (ib + 1) * P], p[:, ib * P : (ib + 1) * P], ident[:])
                nc.vector.tensor_copy(
                    p_t[:, 0 : jb + 1, jb * P : (jb + 1) * P],
                    pt_ps[:, 0 : (jb + 1) * P].rearrange("i (ib j) -> i ib j", j=P),
                )

            def weighted_values(s, head, p_t):
                o_ps = stat_ps.tile([P, T], F32, name="o_ps", tag="stat")
                for ib in range(TB):
                    nc.tensor.matmul(
                        o_ps[:, ib * P : T], v_t[s][:, ib, head * DH : (head + 1) * DH], p_t[:, ib, ib * P : T],
                        start=(ib == 0), stop=(ib == TB - 1),
                    )
                nc.scalar.copy(o[s][:, head, :], o_ps[:])

            def attention(s, groups):
                blocks = H * TB
                order = [(head, jb) for head in range(H) for jb in (range(TB - 1, -1, -1) if head == H - 1 else range(TB))]
                scored, weighed, flipped = {}, {}, {}
                for step in range(max(blocks + FLIP_LAG, len(groups))):
                    if step < blocks:
                        scored[step] = scores(s, *order[step])
                    block = step - WEIGHTS_LAG
                    if 0 <= block < blocks:
                        weighed[block] = weights(*scored[block], (order[block][1] + 1) * P)
                    block = step - FLIP_LAG
                    if 0 <= block < blocks:
                        head, jb = order[block]
                        if block % TB == 0:
                            flipped[head] = soft.tile([P, TB, T], BF16, name="p_t", bufs=2)
                        flip(weighed[block], jb, flipped[head])
                    if step < len(groups):
                        for piece in groups[step]:
                            piece()
                    if 0 <= block < blocks and block % TB == TB - 1:
                        weighted_values(s, block // TB, flipped[block // TB])

            project_qk(0, 0, 0)
            project_v(0, 0)
            project_qk(0, 0, HALF)
            def first_norm():
                layer_norm(h0, channel_mean(h0, 1, stat_ps, three), n1[1], 1, 0, T, 0, stat_ps, by_power=True)

            own = [partial(project_whole, 0, 1, which) for which in (0, 1)]
            own += [partial(project_v, 0, tb) for tb in (1, 2, 3)]
            own += [partial(project_whole, 0, head, which) for head in (2, 3) for which in (0, 1)]
            following = [partial(project_whole, 1, head, which) for head in (0, 1) for which in (0, 1)]
            following += [partial(project_v, 1, tb) for tb in range(TB)]
            following += [partial(project_whole, 1, head, which) for head in (2, 3) for which in (0, 1)]
            groups = [[piece] for piece in own] + [[] for block in range(H * TB - len(own))]
            groups[0] += [first_norm]
            for tb in range(TB):
                groups[(H - 1) * TB + tb] += [following[tb]]
            attention(0, groups)
            for cb in range(CB):
                project_out(0, cb)
            layer_norm(h1, channel_mean(h1, 0, stat_ps), n2[0], 0, 0, T, 2, stat_ps, by_power=True)

            pieces = following[TB:] + [partial(park, fb) for fb in range(PARKED)]
            attention(1, [[piece] for piece in pieces])
            for cb in range(CB):
                project_out(1, cb)
            layer_norm(h1, channel_mean(h1, 1, stat_ps), n2[1], 1, 0, T, 2, stat_ps)

        with tc.tile_pool(name="hidden", bufs=1) as hidden, tc.psum_pool(name="mlp_ps", bufs=4) as mlp_ps:

            def store(s, cb, y_ps, first=0, width=T):
                cols = slice(s * T + first, s * T + first + width)
                y = late.tile([P, width], F32, name="y", bufs=3)
                nc.vector.tensor_tensor(y[:], h1[:, cb, cols], y_ps[:], ALU.add)
                nc.sync.dma_start(out[cb * P : (cb + 1) * P, cols], y[:])

            def mlp_output(s, u):
                for cb in range(CB):
                    parts = ((0, T - P), (T - P, P)) if cb == CB - 1 else ((0, T),)
                    for first, width in parts:
                        y_ps = mlp_ps.tile([P, width], F32, name="y_ps", tag="mlp")
                        for fb in range(FB):
                            nc.tensor.matmul(
                                y_ps[:], fc2_sb[:, fb, cb * P : (cb + 1) * P], u[:, fb, first : first + width],
                                start=(fb == 0), stop=(fb == FB - 1),
                            )
                        store(s, cb, y_ps, first, width)

            sums = [mlp_ps.tile([P, T], F32, name=f"y_ps{cb}", tag="mlp") for cb in range(CB)]
            for fb in range(FB):
                u_first = hidden.tile([P, T], BF16, name="u_first", bufs=FB)
                if fb < PARKED:
                    nc.scalar.activation(u_first[:], parked[:, fb, :], FN.Gelu)
                else:
                    u_ps = qkv_ps.tile([P, T], F32, name="u_ps", tag="qkv")
                    hidden_sums(u_ps, 0, fb)
                    nc.scalar.activation(u_first[:], u_ps[:], FN.Gelu)
                for cb in range(CB):
                    nc.tensor.matmul(
                        sums[cb][:], fc2_sb[:, fb, cb * P : (cb + 1) * P], u_first[:],
                        start=(fb == 0), stop=(fb == FB - 1),
                    )
            for cb in range(CB):
                store(0, cb, sums[cb])

            u_second = hidden.tile([P, FB, T], BF16, name="u_second")
            for fb in range(FB):
                u_ps = qkv_ps.tile([P, T], F32, name="u_ps", tag="qkv")
                hidden_sums(u_ps, 1, fb)
                nc.scalar.activation(u_second[:, fb, :], u_ps[:], FN.Gelu)
            mlp_output(1, u_second)
